import numpy as np
import ml_dtypes


def mxq(x, axis, fmt="e4m3"):
    dtype, down = {"e4m3": (ml_dtypes.float8_e4m3fn, 7), "e5m2": (ml_dtypes.float8_e5m2, 14)}[fmt]
    v = np.moveaxis(np.asarray(x, np.float32).astype(ml_dtypes.bfloat16).astype(np.float64), axis, -1)
    blocks = v.reshape(v.shape[:-1] + (-1, 32))
    amax = np.abs(blocks).max(-1, keepdims=True)
    byte = np.maximum(np.where(amax > 0, np.frexp(amax)[1] - 1 + 127, 0) - down, 1)
    scale = np.exp2(byte - 127.0)
    codes = (blocks / scale).astype(np.float32).astype(dtype).astype(np.float64)
    return np.moveaxis((codes * scale).reshape(v.shape), -1, axis)


WIDE = False


def mx_kscale(k):
    if not WIDE:
        return np.ones(k)
    levels = np.array([10, -10, 5, -5, 0])
    a = np.random.permutation(np.resize(levels, k // 512 * 4)).reshape(k // 512, 4)
    idx = np.arange(k)
    return np.exp2(a[idx // 512, idx % 128 // 32])


BF16 = ml_dtypes.bfloat16


def bf(x):
    return np.asarray(x, np.float32).astype(BF16)


def f64(x):
    return np.asarray(x).astype(np.float64)


B, C, H, W, S = 8, 512, 64, 32, 2
NB = (H // S) * (W // S)


def setup_inputs():
    s = mx_kscale(C)
    return {"x": bf(np.random.standard_normal((B, C, H, W)) * s[None, :, None, None]),
            "Wq": bf(np.random.standard_normal((C, C)) * 1.2 * S / np.sqrt(C) / s[None, :]),
            "bq": bf(np.random.standard_normal(C) * 0.3),
            "Wk": bf(np.random.standard_normal((C, C)) * 1.2 * S / np.sqrt(C) / s[None, :]),
            "bk": bf(np.random.standard_normal(C) * 0.3)}


def reference(x, Wq, bq, Wk, bk):
    x_avg = f64(x).reshape(B, C, H // S, S, W // S, S).mean(axis=(3, 5))
    x_avg = x_avg.reshape(B, C, NB).transpose(0, 2, 1)
    xq = mxq(x_avg, 2, "e4m3")
    Q = (xq @ mxq(f64(Wq), 1, "e4m3").T) + f64(bq)
    K = (xq @ mxq(f64(Wk), 1, "e4m3").T) + f64(bk)
    return Q, K

@@ -1,0 +1,132 @@
+from contextlib import ExitStack
+
+import concourse.masks as masks
+import concourse.mybir as mybir
+
+BF16 = mybir.dt.bfloat16
+F32 = mybir.dt.float32
+U32 = mybir.dt.uint32
+U8 = mybir.dt.uint8
+FP8X4 = mybir.dt.float8_e4m3fn_x4
+ADD = mybir.AluOpType.add
+MULT = mybir.AluOpType.mult
+
+P = 128
+PACK = 4
+B, C, H, W = 8, 512, 64, 32
+BLOCK_ROWS = H // 2
+NB = BLOCK_ROWS * (W // 2)
+N_TILES = NB // P
+O_TILES = C // P
+LOADS_AHEAD = 5
+
+FLOPS = 2 * 2 * B * NB * C * C
+
+
+def quantise_weight(nc, stage, psum, identity, w, codes, scales):
+    w_rows = stage.tile([P, O_TILES, C], BF16)
+    nc.sync.dma_start(out=w_rows[:], in_=w.rearrange("(t r) c -> r t c", r=P))
+    w_words = w_rows[:].bitcast(F32).rearrange("r t (q u) -> r t u q", u=2)
+    w_grouped = stage.tile([P, C, PACK], BF16, align_bytes=64)
+    grouped_words = w_grouped[:].bitcast(F32).rearrange("q (t r) u -> q t r u", r=P)
+    for pair in range(O_TILES // 2):
+        turned = psum.tile([P, 2, 2, P], F32)
+        for t in range(2):
+            for u in range(2):
+                nc.tensor.transpose(turned[:, t, u, :], w_words[:, 2 * pair + t, u, :], identity[:])
+        nc.scalar.copy(
+            out=grouped_words[:, 2 * pair : 2 * pair + 2],
+            in_=turned[:].rearrange("q t u r -> q t r u"),
+        )
+    nc.vector.quantize_mx(
+        out=codes.bitcast(FP8X4),
+        scales=scales,
+        in_=w_grouped[:].rearrange("q o j -> q (o j)"),
+    )
+
+
+def tile_coarseblockattention_pa_t_kernel(tc, x, Wq, bq, Wk, bk, out_0, out_1):
+    nc = tc.nc
+    with ExitStack() as ctx:
+        const = ctx.enter_context(tc.tile_pool(name="const", bufs=1))
+        w_stage = ctx.enter_context(tc.tile_pool(name="w_stage", bufs=2))
+        x_pool = ctx.enter_context(tc.tile_pool(name="x_pool", bufs=LOADS_AHEAD + 1))
+        work = ctx.enter_context(tc.tile_pool(name="work", bufs=2))
+        y_pool = ctx.enter_context(tc.tile_pool(name="y_pool", bufs=4))
+        psum_w = ctx.enter_context(tc.psum_pool(name="psum_w", bufs=2))
+        psum_acc = ctx.enter_context(tc.psum_pool(name="psum_acc", bufs=6))
+
+        x_tiles = {}
+
+        def load_image(b):
+            x_tiles[b] = x_pool.tile([P, PACK, H * W], BF16, name="x_sb")
+            x_b = x[b].rearrange("(p j) h w -> p j (h w)", j=PACK)
+            for half in range(2):
+                js = slice(2 * half, 2 * half + 2)
+                nc.sync.dma_start(out=x_tiles[b][:, js, :], in_=x_b[:, js, :])
+
+        load_image(0)
+
+        identity = const.tile([P, P], F32)
+        masks.make_identity(nc, identity[:])
+        w_codes = const.tile([P, 2, C], U32, align_bytes=64)
+        w_scales = const.tile([P, 2, C], U8, align_bytes=64)
+        bias_all = const.tile([P, 2, C], BF16)
+        for m, (w, bias) in enumerate(((Wq, bq), (Wk, bk))):
+            quantise_weight(nc, w_stage, psum_w, identity, w, w_codes[:, m, :], w_scales[:, m, :])
+            nc.sync.dma_start(out=bias_all[:, m, :], in_=bias.partition_broadcast(P))
+
+        for b in range(1, LOADS_AHEAD):
+            load_image(b)
+
+        for b in range(B):
+            if b + LOADS_AHEAD < B:
+                load_image(b + LOADS_AHEAD)
+            x_sb = x_tiles[b]
+
+            row_sums = work.tile([P, PACK, BLOCK_ROWS * W], F32)
+            for half in range(2):
+                js = slice(2 * half, 2 * half + 2)
+                rows = x_sb[:, js, :].rearrange("p j (r i w) -> p (j r) i w", i=2, w=W)
+                nc.vector.tensor_tensor(
+                    out=row_sums[:, js, :].rearrange("p j (r w) -> p (j r) w", w=W),
+                    in0=rows[:, :, 0, :],
+                    in1=rows[:, :, 1, :],
+                    op=ADD,
+                )
+
+            halves = row_sums[:].rearrange("p j (q t e) -> p e t q j", t=N_TILES, e=2)
+            grouped = work.tile([P, N_TILES, P, PACK], BF16, align_bytes=64)
+            nc.vector.tensor_tensor(out=grouped[:], in0=halves[:, 0], in1=halves[:, 1], op=ADD)
+
+            x_codes = work.tile([P, NB], U32, align_bytes=64)
+            x_scales = work.tile([P, NB], U8, align_bytes=64)
+            nc.vector.quantize_mx(
+                out=x_codes[:].bitcast(FP8X4),
+                scales=x_scales[:],
+                in_=grouped[:].rearrange("p t q j -> p (t q j)"),
+            )
+
+            for m, out in enumerate((out_0, out_1)):
+                y = y_pool.tile([P, N_TILES, C], F32)
+                for t in range(N_TILES):
+                    cols = slice(t * P, (t + 1) * P)
+                    acc = psum_acc.tile([P, C], F32)
+                    nc.tensor.matmul_mx(
+                        out=acc[:],
+                        lhsT=x_codes[:, cols].bitcast(FP8X4),
+                        lhsT_scale=x_scales[:, cols],
+                        rhs=w_codes[:, m, :].bitcast(FP8X4),
+                        rhs_scale=w_scales[:, m, :],
+                        start=True,
+                        stop=True,
+                    )
+                    nc.vector.scalar_tensor_tensor(
+                        out=y[:, t, :],
+                        in0=acc[:],
+                        scalar=0.25,
+                        in1=bias_all[:, m, :],
+                        op0=MULT,
+                        op1=ADD,
+                    )
+                nc.sync.dma_start(out=out[b].rearrange("(q t) o -> q t o", t=N_TILES), in_=y[:])

@@ -95,16 +95,21 @@ def tile_coarseblockattention_pa_t_kernel(tc, x, Wq, bq, Wk, bk, out_0, out_1):
                     op=ADD,
                 )
 
-            halves = row_sums[:].rearrange("p j (q t e) -> p e t q j", t=N_TILES, e=2)
-            grouped = work.tile([P, N_TILES, P, PACK], BF16, align_bytes=64)
-            nc.vector.tensor_tensor(out=grouped[:], in0=halves[:, 0], in1=halves[:, 1], op=ADD)
+            halves = row_sums[:].rearrange("p j (g i e) -> p e g j i", i=4, e=2)
+            grouped = work.tile([P, NB, PACK], BF16, align_bytes=64)
+            nc.vector.tensor_tensor(
+                out=grouped[:].rearrange("p (g i) j -> p g j i", i=4),
+                in0=halves[:, 0],
+                in1=halves[:, 1],
+                op=ADD,
+            )
 
             x_codes = work.tile([P, NB], U32, align_bytes=64)
             x_scales = work.tile([P, NB], U8, align_bytes=64)
             nc.vector.quantize_mx(
                 out=x_codes[:].bitcast(FP8X4),
                 scales=x_scales[:],
-                in_=grouped[:].rearrange("p t q j -> p (t q j)"),
+                in_=grouped[:].rearrange("p n j -> p (n j)"),
             )
 
             for m, out in enumerate((out_0, out_1)):
@@ -129,4 +134,4 @@ def tile_coarseblockattention_pa_t_kernel(tc, x, Wq, bq, Wk, bk, out_0, out_1):
                         op0=MULT,
                         op1=ADD,
                     )
-                nc.sync.dma_start(out=out[b].rearrange("(q t) o -> q t o", t=N_TILES), in_=y[:])
+                nc.sync.dma_start(out=out[b].rearrange("(t q) o -> q t o", q=P), in_=y[:])

@@ -9,7 +9,7 @@ U32 = mybir.dt.uint32
 U8 = mybir.dt.uint8
 FP8X4 = mybir.dt.float8_e4m3fn_x4
 ADD = mybir.AluOpType.add
-MULT = mybir.AluOpType.mult
+IDENTITY = mybir.ActivationFunctionType.Identity
 
 P = 128
 PACK = 4
@@ -19,119 +19,178 @@ NB = BLOCK_ROWS * (W // 2)
 N_TILES = NB // P
 O_TILES = C // P
 LOADS_AHEAD = 5
+UNIT = 2
+UNITS_PER_IMAGE = 2 * O_TILES // UNIT
+UNITS = B * UNITS_PER_IMAGE
 
 FLOPS = 2 * 2 * B * NB * C * C
 
 
-def quantise_weight(nc, stage, psum, identity, w, codes, scales):
-    w_rows = stage.tile([P, O_TILES, C], BF16)
-    nc.sync.dma_start(out=w_rows[:], in_=w.rearrange("(t r) c -> r t c", r=P))
-    w_words = w_rows[:].bitcast(F32).rearrange("r t (q u) -> r t u q", u=2)
-    w_grouped = stage.tile([P, C, PACK], BF16, align_bytes=64)
-    grouped_words = w_grouped[:].bitcast(F32).rearrange("q (t r) u -> q t r u", r=P)
-    for pair in range(O_TILES // 2):
-        turned = psum.tile([P, 2, 2, P], F32)
-        for t in range(2):
-            for u in range(2):
-                nc.tensor.transpose(turned[:, t, u, :], w_words[:, 2 * pair + t, u, :], identity[:])
-        nc.scalar.copy(
-            out=grouped_words[:, 2 * pair : 2 * pair + 2],
-            in_=turned[:].rearrange("q t u r -> q t r u"),
-        )
-    nc.vector.quantize_mx(
-        out=codes.bitcast(FP8X4),
-        scales=scales,
-        in_=w_grouped[:].rearrange("q o j -> q (o j)"),
-    )
-
-
 def tile_coarseblockattention_pa_t_kernel(tc, x, Wq, bq, Wk, bk, out_0, out_1):
     nc = tc.nc
+    weights = (Wq, Wk)
+    biases = (bq, bk)
+    outs = (out_0, out_1)
     with ExitStack() as ctx:
         const = ctx.enter_context(tc.tile_pool(name="const", bufs=1))
         w_stage = ctx.enter_context(tc.tile_pool(name="w_stage", bufs=2))
         x_pool = ctx.enter_context(tc.tile_pool(name="x_pool", bufs=LOADS_AHEAD + 1))
         work = ctx.enter_context(tc.tile_pool(name="work", bufs=2))
-        y_pool = ctx.enter_context(tc.tile_pool(name="y_pool", bufs=4))
-        psum_w = ctx.enter_context(tc.psum_pool(name="psum_w", bufs=2))
-        psum_acc = ctx.enter_context(tc.psum_pool(name="psum_acc", bufs=6))
+        yt_pool = ctx.enter_context(tc.tile_pool(name="yt_pool", bufs=3 * UNIT))
+        y_pool = ctx.enter_context(tc.tile_pool(name="y_pool", bufs=3))
+        psum_acc = ctx.enter_context(tc.psum_pool(name="psum_acc", bufs=2 * UNIT))
+        psum_turn = ctx.enter_context(tc.psum_pool(name="psum_turn", bufs=2 * UNIT))
+        ctx.enter_context(tc.manual_schedule())
 
-        x_tiles = {}
+        x_sb = {}
+        row_sums = {}
+        grouped = {}
+        x_codes = {}
+        x_scales = {}
+        w_rows = {}
+        y_turned = {}
+        y = {}
 
         def load_image(b):
-            x_tiles[b] = x_pool.tile([P, PACK, H * W], BF16, name="x_sb")
+            x_sb[b] = x_pool.tile([P, PACK, H * W], BF16, name="x_sb")
             x_b = x[b].rearrange("(p j) h w -> p j (h w)", j=PACK)
             for half in range(2):
                 js = slice(2 * half, 2 * half + 2)
-                nc.sync.dma_start(out=x_tiles[b][:, js, :], in_=x_b[:, js, :])
+                nc.sync.dma_start(out=x_sb[b][:, js, :], in_=x_b[:, js, :])
 
-        load_image(0)
-
-        identity = const.tile([P, P], F32)
-        masks.make_identity(nc, identity[:])
-        w_codes = const.tile([P, 2, C], U32, align_bytes=64)
-        w_scales = const.tile([P, 2, C], U8, align_bytes=64)
-        bias_all = const.tile([P, 2, C], BF16)
-        for m, (w, bias) in enumerate(((Wq, bq), (Wk, bk))):
-            quantise_weight(nc, w_stage, psum_w, identity, w, w_codes[:, m, :], w_scales[:, m, :])
-            nc.sync.dma_start(out=bias_all[:, m, :], in_=bias.partition_broadcast(P))
-
-        for b in range(1, LOADS_AHEAD):
-            load_image(b)
-
-        for b in range(B):
-            if b + LOADS_AHEAD < B:
-                load_image(b + LOADS_AHEAD)
-            x_sb = x_tiles[b]
-
-            row_sums = work.tile([P, PACK, BLOCK_ROWS * W], F32)
-            for half in range(2):
-                js = slice(2 * half, 2 * half + 2)
-                rows = x_sb[:, js, :].rearrange("p j (r i w) -> p (j r) i w", i=2, w=W)
-                nc.vector.tensor_tensor(
-                    out=row_sums[:, js, :].rearrange("p j (r w) -> p (j r) w", w=W),
-                    in0=rows[:, :, 0, :],
-                    in1=rows[:, :, 1, :],
-                    op=ADD,
-                )
-
-            halves = row_sums[:].rearrange("p j (g i e) -> p e g j i", i=4, e=2)
-            grouped = work.tile([P, NB, PACK], BF16, align_bytes=64)
+        def add_rows(b, half):
+            if half == 0:
+                row_sums[b] = work.tile([P, PACK, BLOCK_ROWS * W], F32, name="row_sums")
+            js = slice(2 * half, 2 * half + 2)
+            rows = x_sb[b][:, js, :].rearrange("p j (r i w) -> p (j r) i w", i=2, w=W)
             nc.vector.tensor_tensor(
-                out=grouped[:].rearrange("p (g i) j -> p g j i", i=4),
+                out=row_sums[b][:, js, :].rearrange("p j (r w) -> p (j r) w", w=W),
+                in0=rows[:, :, 0, :],
+                in1=rows[:, :, 1, :],
+                op=ADD,
+            )
+
+        def add_columns(b):
+            halves = row_sums[b][:].rearrange("p j (g i e) -> p e g j i", i=4, e=2)
+            grouped[b] = work.tile([P, NB, PACK], BF16, align_bytes=64, name="grouped")
+            nc.vector.tensor_tensor(
+                out=grouped[b][:].rearrange("p (g i) j -> p g j i", i=4),
                 in0=halves[:, 0],
                 in1=halves[:, 1],
                 op=ADD,
             )
 
-            x_codes = work.tile([P, NB], U32, align_bytes=64)
-            x_scales = work.tile([P, NB], U8, align_bytes=64)
+        def quantise_image(b):
+            x_codes[b] = work.tile([P, NB], U32, align_bytes=64, name="x_codes")
+            x_scales[b] = work.tile([P, NB], U8, align_bytes=64, name="x_scales")
             nc.vector.quantize_mx(
-                out=x_codes[:].bitcast(FP8X4),
-                scales=x_scales[:],
-                in_=grouped[:].rearrange("p n j -> p (n j)"),
+                out=x_codes[b][:].bitcast(FP8X4),
+                scales=x_scales[b][:],
+                in_=grouped[b][:].rearrange("p n j -> p (n j)"),
             )
 
-            for m, out in enumerate((out_0, out_1)):
-                y = y_pool.tile([P, N_TILES, C], F32)
+        def load_weight(m):
+            w_rows[m] = w_stage.tile([P, O_TILES, C], BF16, name="w_rows")
+            nc.sync.dma_start(out=w_rows[m][:], in_=weights[m].rearrange("(t r) c -> r t c", r=P))
+            nc.sync.dma_start(
+                out=bias_rows[m * O_TILES : (m + 1) * O_TILES, :],
+                in_=biases[m].rearrange("(t r) -> t r", r=P),
+            )
+
+        def quantise_weight(m):
+            w_words = w_rows[m][:].bitcast(F32).rearrange("r t (q u) -> r t u q", u=2)
+            w_grouped = w_stage.tile([P, C, PACK], BF16, align_bytes=64)
+            grouped_words = w_grouped[:].bitcast(F32).rearrange("q (t r) u -> q t r u", r=P)
+            for pair in range(O_TILES // 2):
+                turned = psum_turn.tile([P, 2, 2, P], F32, tag="turned")
+                for t in range(2):
+                    for u in range(2):
+                        nc.tensor.transpose(turned[:, t, u, :], w_words[:, 2 * pair + t, u, :], identity[:])
+                nc.scalar.copy(
+                    out=grouped_words[:, 2 * pair : 2 * pair + 2],
+                    in_=turned[:].rearrange("q t u r -> q t r u"),
+                )
+            nc.vector.quantize_mx(
+                out=w_codes[:, m, :].bitcast(FP8X4),
+                scales=w_scales[:, m, :],
+                in_=w_grouped[:].rearrange("q o j -> q (o j)"),
+            )
+
+        def project(unit):
+            b, m, first = unit // UNITS_PER_IMAGE, unit // (O_TILES // UNIT) % 2, unit * UNIT % O_TILES
+            for o in range(first, first + UNIT):
+                chans = slice(o * P, (o + 1) * P)
+                acc = psum_acc.tile([P, NB], F32)
+                nc.tensor.matmul_mx(
+                    out=acc[:],
+                    lhsT=w_codes[:, m, chans].bitcast(FP8X4),
+                    lhsT_scale=w_scales[:, m, chans],
+                    rhs=x_codes[b][:].bitcast(FP8X4),
+                    rhs_scale=x_scales[b][:],
+                    start=True,
+                    stop=True,
+                )
+                y_turned[unit, o] = yt_pool.tile([P, N_TILES, P], F32, name="y_turned")
+                nc.scalar.activation(
+                    out=y_turned[unit, o][:],
+                    in_=acc[:].rearrange("r (q t) -> r t q", t=N_TILES),
+                    func=IDENTITY,
+                    bias=bias_cols[:, m * O_TILES + o : m * O_TILES + o + 1],
+                    scale=0.25,
+                )
+
+        def turn_back(unit):
+            b, m, first = unit // UNITS_PER_IMAGE, unit // (O_TILES // UNIT) % 2, unit * UNIT % O_TILES
+            if first == 0:
+                y[b, m] = y_pool.tile([P, N_TILES, C], F32, name="y")
+            for o in range(first, first + UNIT):
+                back = psum_turn.tile([P, N_TILES, P], F32, tag="turned")
                 for t in range(N_TILES):
-                    cols = slice(t * P, (t + 1) * P)
-                    acc = psum_acc.tile([P, C], F32)
-                    nc.tensor.matmul_mx(
-                        out=acc[:],
-                        lhsT=x_codes[:, cols].bitcast(FP8X4),
-                        lhsT_scale=x_scales[:, cols],
-                        rhs=w_codes[:, m, :].bitcast(FP8X4),
-                        rhs_scale=w_scales[:, m, :],
-                        start=True,
-                        stop=True,
-                    )
-                    nc.vector.scalar_tensor_tensor(
-                        out=y[:, t, :],
-                        in0=acc[:],
-                        scalar=0.25,
-                        in1=bias_all[:, m, :],
-                        op0=MULT,
-                        op1=ADD,
-                    )
-                nc.sync.dma_start(out=out[b].rearrange("(t q) o -> q t o", q=P), in_=y[:])
+                    nc.tensor.transpose(back[:, t, :], y_turned[unit, o][:, t, :], identity[:])
+                to_vector = o % 2 == 1 if b == B - 1 else o == 1
+                if to_vector:
+                    nc.vector.tensor_copy(out=y[b, m][:, :, o * P : (o + 1) * P], in_=back[:])
+                else:
+                    nc.scalar.copy(out=y[b, m][:, :, o * P : (o + 1) * P], in_=back[:])
+            if first + UNIT == O_TILES:
+                nc.sync.dma_start(out=outs[m][b].rearrange("(q t) o -> q t o", t=N_TILES), in_=y[b, m][:])
+
+        load_image(0)
+        identity = const.tile([P, P], F32)
+        masks.make_identity(nc, identity[:])
+        w_codes = const.tile([P, 2, C], U32, align_bytes=64)
+        w_scales = const.tile([P, 2, C], U8, align_bytes=64)
+        bias_rows = const.tile([P, P], BF16)
+        nc.vector.memset(bias_rows[:], 0.0)
+        load_weight(0)
+        load_weight(1)
+        for b in range(1, LOADS_AHEAD):
+            load_image(b)
+
+        add_rows(0, 0)
+        add_rows(0, 1)
+        add_columns(0)
+        quantise_weight(0)
+        quantise_weight(1)
+        bias_rows_f32 = const.tile([P, P], F32)
+        nc.scalar.copy(out=bias_rows_f32[:], in_=bias_rows[:])
+        bias_turned = psum_turn.tile([P, P], F32, tag="turned")
+        nc.tensor.transpose(bias_turned[:], bias_rows_f32[:], identity[:])
+        bias_cols = const.tile([P, 2 * O_TILES], F32)
+        nc.scalar.copy(out=bias_cols[:], in_=bias_turned[:, 0 : 2 * O_TILES])
+
+        for b in range(B):
+            if b + LOADS_AHEAD < B:
+                load_image(b + LOADS_AHEAD)
+            quantise_image(b)
+            if b + 1 < B:
+                add_rows(b + 1, 0)
+                add_rows(b + 1, 1)
+            for k in range(UNITS_PER_IMAGE):
+                unit = b * UNITS_PER_IMAGE + k
+                if k == UNITS_PER_IMAGE // 2 and b + 1 < B:
+                    add_columns(b + 1)
+                project(unit)
+                if unit > 0:
+                    turn_back(unit - 1)
+        turn_back(UNITS - 1)

@@ -18,7 +18,7 @@ BLOCK_ROWS = H // 2
 NB = BLOCK_ROWS * (W // 2)
 N_TILES = NB // P
 O_TILES = C // P
-LOADS_AHEAD = 5
+LOADS_AHEAD = 3
 UNIT = 2
 UNITS_PER_IMAGE = 2 * O_TILES // UNIT
 UNITS = B * UNITS_PER_IMAGE

@@ -19,6 +19,8 @@ NB = BLOCK_ROWS * (W // 2)
 N_TILES = NB // P
 O_TILES = C // P
 LOADS_AHEAD = 3
+FIRST_PIECES = 4
+PIECES = 2
 UNIT = 2
 UNITS_PER_IMAGE = 2 * O_TILES // UNIT
 UNITS = B * UNITS_PER_IMAGE
@@ -51,17 +53,24 @@ def tile_coarseblockattention_pa_t_kernel(tc, x, Wq, bq, Wk, bk, out_0, out_1):
         y_turned = {}
         y = {}
 
+        def pieces_of(b):
+            return FIRST_PIECES if b == 0 else PIECES
+
+        def channels_of(b, piece):
+            width = PACK // pieces_of(b)
+            return slice(piece * width, (piece + 1) * width)
+
         def load_image(b):
             x_sb[b] = x_pool.tile([P, PACK, H * W], BF16, name="x_sb")
             x_b = x[b].rearrange("(p j) h w -> p j (h w)", j=PACK)
-            for half in range(2):
-                js = slice(2 * half, 2 * half + 2)
+            for piece in range(pieces_of(b)):
+                js = channels_of(b, piece)
                 nc.sync.dma_start(out=x_sb[b][:, js, :], in_=x_b[:, js, :])
 
-        def add_rows(b, half):
-            if half == 0:
+        def add_rows(b, piece):
+            if piece == 0:
                 row_sums[b] = work.tile([P, PACK, BLOCK_ROWS * W], F32, name="row_sums")
-            js = slice(2 * half, 2 * half + 2)
+            js = channels_of(b, piece)
             rows = x_sb[b][:, js, :].rearrange("p j (r i w) -> p (j r) i w", i=2, w=W)
             nc.vector.tensor_tensor(
                 out=row_sums[b][:, js, :].rearrange("p j (r w) -> p (j r) w", w=W),
@@ -147,13 +156,16 @@ def tile_coarseblockattention_pa_t_kernel(tc, x, Wq, bq, Wk, bk, out_0, out_1):
                 back = psum_turn.tile([P, N_TILES, P], F32, tag="turned")
                 for t in range(N_TILES):
                     nc.tensor.transpose(back[:, t, :], y_turned[unit, o][:, t, :], identity[:])
-                to_vector = o % 2 == 1 if b == B - 1 else o == 1
-                if to_vector:
+                if b == B - 1 or o == 1:
                     nc.vector.tensor_copy(out=y[b, m][:, :, o * P : (o + 1) * P], in_=back[:])
                 else:
                     nc.scalar.copy(out=y[b, m][:, :, o * P : (o + 1) * P], in_=back[:])
-            if first + UNIT == O_TILES:
-                nc.sync.dma_start(out=outs[m][b].rearrange("(q t) o -> q t o", t=N_TILES), in_=y[b, m][:])
+            out_rows = outs[m][b].rearrange("(q t) o -> q t o", t=N_TILES)
+            if b == B - 1:
+                chans = slice(first * P, (first + UNIT) * P)
+                nc.sync.dma_start(out=out_rows[:, :, chans], in_=y[b, m][:, :, chans])
+            elif first + UNIT == O_TILES:
+                nc.sync.dma_start(out=out_rows, in_=y[b, m][:])
 
         load_image(0)
         identity = const.tile([P, P], F32)
@@ -167,10 +179,11 @@ def tile_coarseblockattention_pa_t_kernel(tc, x, Wq, bq, Wk, bk, out_0, out_1):
         for b in range(1, LOADS_AHEAD):
             load_image(b)
 
-        add_rows(0, 0)
-        add_rows(0, 1)
+        for piece in range(pieces_of(0)):
+            add_rows(0, piece)
         add_columns(0)
         quantise_weight(0)
+        quantise_image(0)
         quantise_weight(1)
         bias_rows_f32 = const.tile([P, P], F32)
         nc.scalar.copy(out=bias_rows_f32[:], in_=bias_rows[:])
@@ -182,10 +195,9 @@ def tile_coarseblockattention_pa_t_kernel(tc, x, Wq, bq, Wk, bk, out_0, out_1):
         for b in range(B):
             if b + LOADS_AHEAD < B:
                 load_image(b + LOADS_AHEAD)
-            quantise_image(b)
             if b + 1 < B:
-                add_rows(b + 1, 0)
-                add_rows(b + 1, 1)
+                for piece in range(pieces_of(b + 1)):
+                    add_rows(b + 1, piece)
             for k in range(UNITS_PER_IMAGE):
                 unit = b * UNITS_PER_IMAGE + k
                 if k == UNITS_PER_IMAGE // 2 and b + 1 < B:
@@ -193,4 +205,6 @@ def tile_coarseblockattention_pa_t_kernel(tc, x, Wq, bq, Wk, bk, out_0, out_1):
                 project(unit)
                 if unit > 0:
                     turn_back(unit - 1)
+            if b + 1 < B:
+                quantise_image(b + 1)
         turn_back(UNITS - 1)

@@ -13,7 +13,9 @@ IDENTITY = mybir.ActivationFunctionType.Identity
 
 P = 128
 PACK = 4
+WORDS = 2
 B, C, H, W = 8, 512, 64, 32
+PIXELS = 4
 BLOCK_ROWS = H // 2
 NB = BLOCK_ROWS * (W // 2)
 N_TILES = NB // P
@@ -24,6 +26,7 @@ PIECES = 2
 UNIT = 2
 UNITS_PER_IMAGE = 2 * O_TILES // UNIT
 UNITS = B * UNITS_PER_IMAGE
+VECTOR_TILE = 3
 
 FLOPS = 2 * 2 * B * NB * C * C
 
@@ -71,19 +74,19 @@ def tile_coarseblockattention_pa_t_kernel(tc, x, Wq, bq, Wk, bk, out_0, out_1):
             if piece == 0:
                 row_sums[b] = work.tile([P, PACK, BLOCK_ROWS * W], F32, name="row_sums")
             js = channels_of(b, piece)
-            rows = x_sb[b][:, js, :].rearrange("p j (r i w) -> p (j r) i w", i=2, w=W)
+            rows = x_sb[b][:, js, :].rearrange("p j (v i w) -> p (j v) i w", i=2, w=W)
             nc.vector.tensor_tensor(
-                out=row_sums[b][:, js, :].rearrange("p j (r w) -> p (j r) w", w=W),
+                out=row_sums[b][:, js, :].rearrange("p j (v w) -> p (j v) w", w=W),
                 in0=rows[:, :, 0, :],
                 in1=rows[:, :, 1, :],
                 op=ADD,
             )
 
         def add_columns(b):
-            halves = row_sums[b][:].rearrange("p j (g i e) -> p e g j i", i=4, e=2)
+            halves = row_sums[b][:].rearrange("p j (q t e) -> p e q j t", t=N_TILES, e=2)
             grouped[b] = work.tile([P, NB, PACK], BF16, align_bytes=64, name="grouped")
             nc.vector.tensor_tensor(
-                out=grouped[b][:].rearrange("p (g i) j -> p g j i", i=4),
+                out=grouped[b][:].rearrange("p (q t) j -> p q j t", t=N_TILES),
                 in0=halves[:, 0],
                 in1=halves[:, 1],
                 op=ADD,
@@ -100,33 +103,36 @@ def tile_coarseblockattention_pa_t_kernel(tc, x, Wq, bq, Wk, bk, out_0, out_1):
 
         def load_weight(m):
             w_rows[m] = w_stage.tile([P, O_TILES, C], BF16, name="w_rows")
-            nc.sync.dma_start(out=w_rows[m][:], in_=weights[m].rearrange("(t r) c -> r t c", r=P))
+            nc.sync.dma_start(out=w_rows[m][:], in_=weights[m].rearrange("(o r) c -> r o c", r=P))
             nc.sync.dma_start(
                 out=bias_rows[m * O_TILES : (m + 1) * O_TILES, :],
-                in_=biases[m].rearrange("(t r) -> t r", r=P),
+                in_=biases[m].rearrange("(o r) -> o r", r=P),
             )
 
         def quantise_weight(m):
-            w_words = w_rows[m][:].bitcast(F32).rearrange("r t (q u) -> r t u q", u=2)
+            w_words = w_rows[m][:].bitcast(F32).rearrange("r o (p u) -> r o u p", u=WORDS)
             w_grouped = w_stage.tile([P, C, PACK], BF16, align_bytes=64)
-            grouped_words = w_grouped[:].bitcast(F32).rearrange("q (t r) u -> q t r u", r=P)
+            grouped_words = w_grouped[:].bitcast(F32).rearrange("p (o r) u -> p o r u", r=P)
             for pair in range(O_TILES // 2):
-                turned = psum_turn.tile([P, 2, 2, P], F32, tag="turned")
-                for t in range(2):
-                    for u in range(2):
-                        nc.tensor.transpose(turned[:, t, u, :], w_words[:, 2 * pair + t, u, :], identity[:])
+                turned = psum_turn.tile([P, 2, WORDS, P], F32, tag="turned")
+                for o in range(2):
+                    for u in range(WORDS):
+                        nc.tensor.transpose(turned[:, o, u, :], w_words[:, 2 * pair + o, u, :], identity[:])
                 nc.scalar.copy(
                     out=grouped_words[:, 2 * pair : 2 * pair + 2],
-                    in_=turned[:].rearrange("q t u r -> q t r u"),
+                    in_=turned[:].rearrange("p o u r -> p o r u"),
                 )
             nc.vector.quantize_mx(
                 out=w_codes[:, m, :].bitcast(FP8X4),
                 scales=w_scales[:, m, :],
-                in_=w_grouped[:].rearrange("q o j -> q (o j)"),
+                in_=w_grouped[:].rearrange("p c j -> p (c j)"),
             )
 
+        def parts_of(unit):
+            return unit // UNITS_PER_IMAGE, unit // (O_TILES // UNIT) % 2, unit * UNIT % O_TILES
+
         def project(unit):
-            b, m, first = unit // UNITS_PER_IMAGE, unit // (O_TILES // UNIT) % 2, unit * UNIT % O_TILES
+            b, m, first = parts_of(unit)
             for o in range(first, first + UNIT):
                 chans = slice(o * P, (o + 1) * P)
                 acc = psum_acc.tile([P, NB], F32)
@@ -145,22 +151,22 @@ def tile_coarseblockattention_pa_t_kernel(tc, x, Wq, bq, Wk, bk, out_0, out_1):
                     in_=acc[:].rearrange("r (q t) -> r t q", t=N_TILES),
                     func=IDENTITY,
                     bias=bias_cols[:, m * O_TILES + o : m * O_TILES + o + 1],
-                    scale=0.25,
+                    scale=1.0 / PIXELS,
                 )
 
         def turn_back(unit):
-            b, m, first = unit // UNITS_PER_IMAGE, unit // (O_TILES // UNIT) % 2, unit * UNIT % O_TILES
+            b, m, first = parts_of(unit)
             if first == 0:
                 y[b, m] = y_pool.tile([P, N_TILES, C], F32, name="y")
             for o in range(first, first + UNIT):
                 back = psum_turn.tile([P, N_TILES, P], F32, tag="turned")
                 for t in range(N_TILES):
                     nc.tensor.transpose(back[:, t, :], y_turned[unit, o][:, t, :], identity[:])
-                if b == B - 1 or o == 1:
+                if b == B - 1 or o == VECTOR_TILE:
                     nc.vector.tensor_copy(out=y[b, m][:, :, o * P : (o + 1) * P], in_=back[:])
                 else:
                     nc.scalar.copy(out=y[b, m][:, :, o * P : (o + 1) * P], in_=back[:])
-            out_rows = outs[m][b].rearrange("(q t) o -> q t o", t=N_TILES)
+            out_rows = outs[m][b].rearrange("(q t) c -> q t c", t=N_TILES)
             if b == B - 1:
                 chans = slice(first * P, (first + UNIT) * P)
                 nc.sync.dma_start(out=out_rows[:, :, chans], in_=y[b, m][:, :, chans])

@@ -9,6 +9,7 @@ U32 = mybir.dt.uint32
 U8 = mybir.dt.uint8
 FP8X4 = mybir.dt.float8_e4m3fn_x4
 ADD = mybir.AluOpType.add
+MULT = mybir.AluOpType.mult
 IDENTITY = mybir.ActivationFunctionType.Identity
 
 P = 128
@@ -18,7 +19,10 @@ B, C, H, W = 8, 512, 64, 32
 PIXELS = 4
 BLOCK_ROWS = H // 2
 NB = BLOCK_ROWS * (W // 2)
-N_TILES = NB // P
+DIRECT_FROM = NB - P
+ROWS = DIRECT_FROM // P
+WIDE = 256
+PE_POOLED_IMAGES = 6
 O_TILES = C // P
 LOADS_AHEAD = 3
 FIRST_PIECES = 4
@@ -26,7 +30,6 @@ PIECES = 2
 UNIT = 2
 UNITS_PER_IMAGE = 2 * O_TILES // UNIT
 UNITS = B * UNITS_PER_IMAGE
-VECTOR_TILE = 3
 
 FLOPS = 2 * 2 * B * NB * C * C
 
@@ -43,8 +46,10 @@ def tile_coarseblockattention_pa_t_kernel(tc, x, Wq, bq, Wk, bk, out_0, out_1):
         work = ctx.enter_context(tc.tile_pool(name="work", bufs=2))
         yt_pool = ctx.enter_context(tc.tile_pool(name="yt_pool", bufs=3 * UNIT))
         y_pool = ctx.enter_context(tc.tile_pool(name="y_pool", bufs=3))
-        psum_acc = ctx.enter_context(tc.psum_pool(name="psum_acc", bufs=2 * UNIT))
-        psum_turn = ctx.enter_context(tc.psum_pool(name="psum_turn", bufs=2 * UNIT))
+        yd_pool = ctx.enter_context(tc.tile_pool(name="yd_pool", bufs=4))
+        psum_acc = ctx.enter_context(tc.psum_pool(name="psum_acc", bufs=3))
+        psum_turn = ctx.enter_context(tc.psum_pool(name="psum_turn", bufs=3))
+        psum_side = ctx.enter_context(tc.psum_pool(name="psum_side", bufs=2))
         ctx.enter_context(tc.manual_schedule())
 
         x_sb = {}
@@ -55,6 +60,8 @@ def tile_coarseblockattention_pa_t_kernel(tc, x, Wq, bq, Wk, bk, out_0, out_1):
         w_rows = {}
         y_turned = {}
         y = {}
+        acc_direct = {}
+        pooled = {}
 
         def pieces_of(b):
             return FIRST_PIECES if b == 0 else PIECES
@@ -70,23 +77,46 @@ def tile_coarseblockattention_pa_t_kernel(tc, x, Wq, bq, Wk, bk, out_0, out_1):
                 js = channels_of(b, piece)
                 nc.sync.dma_start(out=x_sb[b][:, js, :], in_=x_b[:, js, :])
 
+        def vector_blocks(b):
+            return DIRECT_FROM if b < PE_POOLED_IMAGES else NB
+
+        def pool_on_tensor(b):
+            pooled[b] = psum_side.tile([P, PACK, P], F32, tag="side", name="pooled")
+            pixels = x_sb[b][:, :, PIXELS * DIRECT_FROM : PIXELS * NB].rearrange(
+                "p j (v i w e) -> p i e j v w", i=2, w=W // 2, e=2
+            )
+            for i in range(2):
+                for e in range(2):
+                    nc.tensor.matmul(
+                        out=pooled[b][:].rearrange("p j n -> p (j n)"),
+                        lhsT=identity_bf16[:],
+                        rhs=pixels[:, i, e],
+                        start=(i == 0 and e == 0),
+                        stop=(i == 1 and e == 1),
+                    )
+
+        def round_pooled(b):
+            nc.scalar.copy(out=grouped[b][:, DIRECT_FROM:NB, :], in_=pooled[b][:].rearrange("p j n -> p n j"))
+
         def add_rows(b, piece):
             if piece == 0:
                 row_sums[b] = work.tile([P, PACK, BLOCK_ROWS * W], F32, name="row_sums")
+                grouped[b] = work.tile([P, NB, PACK], BF16, align_bytes=64, name="grouped")
             js = channels_of(b, piece)
-            rows = x_sb[b][:, js, :].rearrange("p j (v i w) -> p (j v) i w", i=2, w=W)
+            block_rows = vector_blocks(b) // (W // 2)
+            rows = x_sb[b][:, js, 0 : block_rows * 2 * W].rearrange("p j (v i w) -> p j v i w", i=2, w=W)
             nc.vector.tensor_tensor(
-                out=row_sums[b][:, js, :].rearrange("p j (v w) -> p (j v) w", w=W),
-                in0=rows[:, :, 0, :],
-                in1=rows[:, :, 1, :],
+                out=row_sums[b][:, js, 0 : block_rows * W].rearrange("p j (v w) -> p j v w", w=W),
+                in0=rows[:, :, :, 0, :],
+                in1=rows[:, :, :, 1, :],
                 op=ADD,
             )
 
         def add_columns(b):
-            halves = row_sums[b][:].rearrange("p j (q t e) -> p e q j t", t=N_TILES, e=2)
-            grouped[b] = work.tile([P, NB, PACK], BF16, align_bytes=64, name="grouped")
+            blocks = vector_blocks(b)
+            halves = row_sums[b][:, :, 0 : 2 * blocks].rearrange("p j (q t e) -> p e q j t", t=PACK, e=2)
             nc.vector.tensor_tensor(
-                out=grouped[b][:].rearrange("p (q t) j -> p q j t", t=N_TILES),
+                out=grouped[b][:, 0:blocks, :].rearrange("p (q t) j -> p q j t", t=PACK),
                 in0=halves[:, 0],
                 in1=halves[:, 1],
                 op=ADD,
@@ -136,19 +166,20 @@ def tile_coarseblockattention_pa_t_kernel(tc, x, Wq, bq, Wk, bk, out_0, out_1):
             for o in range(first, first + UNIT):
                 chans = slice(o * P, (o + 1) * P)
                 acc = psum_acc.tile([P, NB], F32)
-                nc.tensor.matmul_mx(
-                    out=acc[:],
-                    lhsT=w_codes[:, m, chans].bitcast(FP8X4),
-                    lhsT_scale=w_scales[:, m, chans],
-                    rhs=x_codes[b][:].bitcast(FP8X4),
-                    rhs_scale=x_scales[b][:],
-                    start=True,
-                    stop=True,
-                )
-                y_turned[unit, o] = yt_pool.tile([P, N_TILES, P], F32, name="y_turned")
+                for blocks in (slice(0, WIDE), slice(WIDE, DIRECT_FROM)):
+                    nc.tensor.matmul_mx(
+                        out=acc[:, blocks],
+                        lhsT=w_codes[:, m, chans].bitcast(FP8X4),
+                        lhsT_scale=w_scales[:, m, chans],
+                        rhs=x_codes[b][:, blocks].bitcast(FP8X4),
+                        rhs_scale=x_scales[b][:, blocks],
+                        start=True,
+                        stop=True,
+                    )
+                y_turned[unit, o] = yt_pool.tile([P, ROWS, P], F32, name="y_turned")
                 nc.scalar.activation(
                     out=y_turned[unit, o][:],
-                    in_=acc[:].rearrange("r (q t) -> r t q", t=N_TILES),
+                    in_=acc[:, 0:DIRECT_FROM].rearrange("r (q t) -> r t q", t=ROWS),
                     func=IDENTITY,
                     bias=bias_cols[:, m * O_TILES + o : m * O_TILES + o + 1],
                     scale=1.0 / PIXELS,
@@ -157,25 +188,51 @@ def tile_coarseblockattention_pa_t_kernel(tc, x, Wq, bq, Wk, bk, out_0, out_1):
         def turn_back(unit):
             b, m, first = parts_of(unit)
             if first == 0:
-                y[b, m] = y_pool.tile([P, N_TILES, C], F32, name="y")
+                y[b, m] = y_pool.tile([P, ROWS, C], F32, name="y")
             for o in range(first, first + UNIT):
-                back = psum_turn.tile([P, N_TILES, P], F32, tag="turned")
-                for t in range(N_TILES):
+                back = psum_turn.tile([P, ROWS, P], F32, tag="turned")
+                for t in range(ROWS):
                     nc.tensor.transpose(back[:, t, :], y_turned[unit, o][:, t, :], identity[:])
-                if b == B - 1 or o == VECTOR_TILE:
+                if b == B - 1:
                     nc.vector.tensor_copy(out=y[b, m][:, :, o * P : (o + 1) * P], in_=back[:])
                 else:
                     nc.scalar.copy(out=y[b, m][:, :, o * P : (o + 1) * P], in_=back[:])
-            out_rows = outs[m][b].rearrange("(q t) c -> q t c", t=N_TILES)
+            out_rows = outs[m][b][0:DIRECT_FROM].rearrange("(q t) c -> q t c", t=ROWS)
             if b == B - 1:
                 chans = slice(first * P, (first + UNIT) * P)
                 nc.sync.dma_start(out=out_rows[:, :, chans], in_=y[b, m][:, :, chans])
             elif first + UNIT == O_TILES:
                 nc.sync.dma_start(out=out_rows, in_=y[b, m][:])
 
+        def project_direct(b, m):
+            acc_direct[b, m] = psum_side.tile([P, C], F32, tag="side", name="acc_direct")
+            nc.tensor.matmul_mx(
+                out=acc_direct[b, m][:],
+                lhsT=x_codes[b][:, DIRECT_FROM:NB].bitcast(FP8X4),
+                lhsT_scale=x_scales[b][:, DIRECT_FROM:NB],
+                rhs=w_codes[:, m, :].bitcast(FP8X4),
+                rhs_scale=w_scales[:, m, :],
+                start=True,
+                stop=True,
+            )
+
+        def finish_direct(b, m):
+            y_direct = yd_pool.tile([P, C], F32, name="y_direct")
+            nc.vector.scalar_tensor_tensor(
+                out=y_direct[:],
+                in0=acc_direct[b, m][:],
+                scalar=1.0 / PIXELS,
+                in1=bias_all[:, m, :],
+                op0=MULT,
+                op1=ADD,
+            )
+            nc.sync.dma_start(out=outs[m][b][DIRECT_FROM:NB, :], in_=y_direct[:])
+
         load_image(0)
         identity = const.tile([P, P], F32)
         masks.make_identity(nc, identity[:])
+        identity_bf16 = const.tile([P, P], BF16)
+        masks.make_identity(nc, identity_bf16[:])
         w_codes = const.tile([P, 2, C], U32, align_bytes=64)
         w_scales = const.tile([P, 2, C], U8, align_bytes=64)
         bias_rows = const.tile([P, P], BF16)
@@ -187,6 +244,8 @@ def tile_coarseblockattention_pa_t_kernel(tc, x, Wq, bq, Wk, bk, out_0, out_1):
 
         for piece in range(pieces_of(0)):
             add_rows(0, piece)
+        pool_on_tensor(0)
+        round_pooled(0)
         add_columns(0)
         quantise_weight(0)
         quantise_image(0)
@@ -197,6 +256,13 @@ def tile_coarseblockattention_pa_t_kernel(tc, x, Wq, bq, Wk, bk, out_0, out_1):
         nc.tensor.transpose(bias_turned[:], bias_rows_f32[:], identity[:])
         bias_cols = const.tile([P, 2 * O_TILES], F32)
         nc.scalar.copy(out=bias_cols[:], in_=bias_turned[:, 0 : 2 * O_TILES])
+        bias_all = const.tile([P, 2, C], F32)
+        for m in range(2):
+            spread = psum_turn.tile([P, O_TILES, P], F32, tag="turned")
+            for o in range(O_TILES):
+                col = m * O_TILES + o
+                nc.tensor.transpose(spread[:, o, :], bias_cols[:, col : col + 1].to_broadcast([P, P]), identity[:])
+            nc.scalar.copy(out=bias_all[:, m, :], in_=spread[:].rearrange("q o r -> q (o r)"))
 
         for b in range(B):
             if b + LOADS_AHEAD < B:
@@ -209,8 +275,16 @@ def tile_coarseblockattention_pa_t_kernel(tc, x, Wq, bq, Wk, bk, out_0, out_1):
                 if k == UNITS_PER_IMAGE // 2 and b + 1 < B:
                     add_columns(b + 1)
                 project(unit)
+                if k == 0 and b + 1 < PE_POOLED_IMAGES:
+                    pool_on_tensor(b + 1)
+                if k % 2 == 0:
+                    project_direct(b, k // 2)
                 if unit > 0:
                     turn_back(unit - 1)
+                if k == 0 and b + 1 < PE_POOLED_IMAGES:
+                    round_pooled(b + 1)
+                if k % 2 == 0:
+                    finish_direct(b, k // 2)
             if b + 1 < B:
                 quantise_image(b + 1)
         turn_back(UNITS - 1)

@@ -24,7 +24,7 @@ ROWS = DIRECT_FROM // P
 WIDE = 256
 PE_POOLED_IMAGES = 6
 O_TILES = C // P
-LOADS_AHEAD = 3
+LOADS_AHEAD = 4
 FIRST_PIECES = 4
 PIECES = 2
 UNIT = 2
@@ -45,8 +45,8 @@ def tile_coarseblockattention_pa_t_kernel(tc, x, Wq, bq, Wk, bk, out_0, out_1):
         x_pool = ctx.enter_context(tc.tile_pool(name="x_pool", bufs=LOADS_AHEAD + 1))
         work = ctx.enter_context(tc.tile_pool(name="work", bufs=2))
         yt_pool = ctx.enter_context(tc.tile_pool(name="yt_pool", bufs=3 * UNIT))
-        y_pool = ctx.enter_context(tc.tile_pool(name="y_pool", bufs=3))
-        yd_pool = ctx.enter_context(tc.tile_pool(name="yd_pool", bufs=4))
+        y_pool = ctx.enter_context(tc.tile_pool(name="y_pool", bufs=7))
+        yd_pool = ctx.enter_context(tc.tile_pool(name="yd_pool", bufs=8))
         psum_acc = ctx.enter_context(tc.psum_pool(name="psum_acc", bufs=3))
         psum_turn = ctx.enter_context(tc.psum_pool(name="psum_turn", bufs=3))
         psum_side = ctx.enter_context(tc.psum_pool(name="psum_side", bufs=2))

@@ -22,7 +22,7 @@ NB = BLOCK_ROWS * (W // 2)
 DIRECT_FROM = NB - P
 ROWS = DIRECT_FROM // P
 WIDE = 256
-PE_POOLED_IMAGES = 6
+TENSOR_POOLS_FROM = NB - 96
 O_TILES = C // P
 LOADS_AHEAD = 4
 FIRST_PIECES = 4
@@ -78,11 +78,11 @@ def tile_coarseblockattention_pa_t_kernel(tc, x, Wq, bq, Wk, bk, out_0, out_1):
                 nc.sync.dma_start(out=x_sb[b][:, js, :], in_=x_b[:, js, :])
 
         def vector_blocks(b):
-            return DIRECT_FROM if b < PE_POOLED_IMAGES else NB
+            return TENSOR_POOLS_FROM
 
         def pool_on_tensor(b):
-            pooled[b] = psum_side.tile([P, PACK, P], F32, tag="side", name="pooled")
-            pixels = x_sb[b][:, :, PIXELS * DIRECT_FROM : PIXELS * NB].rearrange(
+            pooled[b] = psum_side.tile([P, PACK, NB - TENSOR_POOLS_FROM], F32, tag="side", name="pooled")
+            pixels = x_sb[b][:, :, PIXELS * TENSOR_POOLS_FROM : PIXELS * NB].rearrange(
                 "p j (v i w e) -> p i e j v w", i=2, w=W // 2, e=2
             )
             for i in range(2):
@@ -96,7 +96,7 @@ def tile_coarseblockattention_pa_t_kernel(tc, x, Wq, bq, Wk, bk, out_0, out_1):
                     )
 
         def round_pooled(b):
-            nc.scalar.copy(out=grouped[b][:, DIRECT_FROM:NB, :], in_=pooled[b][:].rearrange("p j n -> p n j"))
+            nc.scalar.copy(out=grouped[b][:, TENSOR_POOLS_FROM:NB, :], in_=pooled[b][:].rearrange("p j n -> p n j"))
 
         def add_rows(b, piece):
             if piece == 0:
@@ -275,13 +275,13 @@ def tile_coarseblockattention_pa_t_kernel(tc, x, Wq, bq, Wk, bk, out_0, out_1):
                 if k == UNITS_PER_IMAGE // 2 and b + 1 < B:
                     add_columns(b + 1)
                 project(unit)
-                if k == 0 and b + 1 < PE_POOLED_IMAGES:
+                if k == 0 and b + 1 < B:
                     pool_on_tensor(b + 1)
                 if k % 2 == 0:
                     project_direct(b, k // 2)
                 if unit > 0:
                     turn_back(unit - 1)
-                if k == 0 and b + 1 < PE_POOLED_IMAGES:
+                if k == 0 and b + 1 < B:
                     round_pooled(b + 1)
                 if k % 2 == 0:
                     finish_direct(b, k // 2)

@@ -19,17 +19,22 @@ B, C, H, W = 8, 512, 64, 32
 PIXELS = 4
 BLOCK_ROWS = H // 2
 NB = BLOCK_ROWS * (W // 2)
-DIRECT_FROM = NB - P
-ROWS = DIRECT_FROM // P
-WIDE = 256
-TENSOR_POOLS_FROM = NB - 96
+N_TILES = NB // P
 O_TILES = C // P
+TENSOR_POOLS_FROM = NB - 96
+TURNED = ((0, 0), (0, 1), (0, 2), (0, 3), (1, 0), (1, 1))
+DIRECT_M = 1
+DIRECT_FROM = 2 * P
+DIRECT_WIDTH = C - DIRECT_FROM
+HALVES = 2
 LOADS_AHEAD = 4
 FIRST_PIECES = 4
 PIECES = 2
 UNIT = 2
-UNITS_PER_IMAGE = 2 * O_TILES // UNIT
+UNITS_PER_IMAGE = len(TURNED) // UNIT
 UNITS = B * UNITS_PER_IMAGE
+ACC_BANKS = 3
+TURN_BANKS = 2
 
 FLOPS = 2 * 2 * B * NB * C * C
 
@@ -45,11 +50,11 @@ def tile_coarseblockattention_pa_t_kernel(tc, x, Wq, bq, Wk, bk, out_0, out_1):
         x_pool = ctx.enter_context(tc.tile_pool(name="x_pool", bufs=LOADS_AHEAD + 1))
         work = ctx.enter_context(tc.tile_pool(name="work", bufs=2))
         yt_pool = ctx.enter_context(tc.tile_pool(name="yt_pool", bufs=3 * UNIT))
-        y_pool = ctx.enter_context(tc.tile_pool(name="y_pool", bufs=7))
-        yd_pool = ctx.enter_context(tc.tile_pool(name="yd_pool", bufs=8))
-        psum_acc = ctx.enter_context(tc.psum_pool(name="psum_acc", bufs=3))
-        psum_turn = ctx.enter_context(tc.psum_pool(name="psum_turn", bufs=3))
-        psum_side = ctx.enter_context(tc.psum_pool(name="psum_side", bufs=2))
+        y_pool = ctx.enter_context(tc.tile_pool(name="y_pool", bufs=6))
+        psum_acc = ctx.enter_context(tc.psum_pool(name="psum_acc", bufs=ACC_BANKS))
+        psum_turn = ctx.enter_context(tc.psum_pool(name="psum_turn", bufs=TURN_BANKS))
+        psum_direct = ctx.enter_context(tc.psum_pool(name="psum_direct", bufs=HALVES))
+        psum_pooled = ctx.enter_context(tc.psum_pool(name="psum_pooled", bufs=1))
         ctx.enter_context(tc.manual_schedule())
 
         x_sb = {}
@@ -77,11 +82,8 @@ def tile_coarseblockattention_pa_t_kernel(tc, x, Wq, bq, Wk, bk, out_0, out_1):
                 js = channels_of(b, piece)
                 nc.sync.dma_start(out=x_sb[b][:, js, :], in_=x_b[:, js, :])
 
-        def vector_blocks(b):
-            return TENSOR_POOLS_FROM
-
         def pool_on_tensor(b):
-            pooled[b] = psum_side.tile([P, PACK, NB - TENSOR_POOLS_FROM], F32, tag="side", name="pooled")
+            pooled[b] = psum_pooled.tile([P, PACK, NB - TENSOR_POOLS_FROM], F32, name="pooled")
             pixels = x_sb[b][:, :, PIXELS * TENSOR_POOLS_FROM : PIXELS * NB].rearrange(
                 "p j (v i w e) -> p i e j v w", i=2, w=W // 2, e=2
             )
@@ -103,7 +105,7 @@ def tile_coarseblockattention_pa_t_kernel(tc, x, Wq, bq, Wk, bk, out_0, out_1):
                 row_sums[b] = work.tile([P, PACK, BLOCK_ROWS * W], F32, name="row_sums")
                 grouped[b] = work.tile([P, NB, PACK], BF16, align_bytes=64, name="grouped")
             js = channels_of(b, piece)
-            block_rows = vector_blocks(b) // (W // 2)
+            block_rows = TENSOR_POOLS_FROM // (W // 2)
             rows = x_sb[b][:, js, 0 : block_rows * 2 * W].rearrange("p j (v i w) -> p j v i w", i=2, w=W)
             nc.vector.tensor_tensor(
                 out=row_sums[b][:, js, 0 : block_rows * W].rearrange("p j (v w) -> p j v w", w=W),
@@ -113,10 +115,9 @@ def tile_coarseblockattention_pa_t_kernel(tc, x, Wq, bq, Wk, bk, out_0, out_1):
             )
 
         def add_columns(b):
-            blocks = vector_blocks(b)
-            halves = row_sums[b][:, :, 0 : 2 * blocks].rearrange("p j (q t e) -> p e q j t", t=PACK, e=2)
+            halves = row_sums[b][:, :, 0 : 2 * TENSOR_POOLS_FROM].rearrange("p j (g s e) -> p e g j s", s=PACK, e=2)
             nc.vector.tensor_tensor(
-                out=grouped[b][:, 0:blocks, :].rearrange("p (q t) j -> p q j t", t=PACK),
+                out=grouped[b][:, 0:TENSOR_POOLS_FROM, :].rearrange("p (g s) j -> p g j s", s=PACK),
                 in0=halves[:, 0],
                 in1=halves[:, 1],
                 op=ADD,
@@ -158,75 +159,84 @@ def tile_coarseblockattention_pa_t_kernel(tc, x, Wq, bq, Wk, bk, out_0, out_1):
                 in_=w_grouped[:].rearrange("p c j -> p (c j)"),
             )
 
-        def parts_of(unit):
-            return unit // UNITS_PER_IMAGE, unit // (O_TILES // UNIT) % 2, unit * UNIT % O_TILES
+        def result(b, m):
+            if (b, m) not in y:
+                y[b, m] = y_pool.tile([P, N_TILES, C], F32, name="y")
+            return y[b, m]
+
+        def store(b, m, chans):
+            out_rows = outs[m][b].rearrange("(t q) c -> q t c", q=P)
+            nc.sync.dma_start(out=out_rows[:, :, chans], in_=result(b, m)[:, :, chans])
+
+        def tiles_of(unit):
+            first = unit % UNITS_PER_IMAGE * UNIT
+            return unit // UNITS_PER_IMAGE, TURNED[first : first + UNIT]
 
         def project(unit):
-            b, m, first = parts_of(unit)
-            for o in range(first, first + UNIT):
+            b, tiles = tiles_of(unit)
+            for m, o in tiles:
                 chans = slice(o * P, (o + 1) * P)
                 acc = psum_acc.tile([P, NB], F32)
-                for blocks in (slice(0, WIDE), slice(WIDE, DIRECT_FROM)):
-                    nc.tensor.matmul_mx(
-                        out=acc[:, blocks],
-                        lhsT=w_codes[:, m, chans].bitcast(FP8X4),
-                        lhsT_scale=w_scales[:, m, chans],
-                        rhs=x_codes[b][:, blocks].bitcast(FP8X4),
-                        rhs_scale=x_scales[b][:, blocks],
-                        start=True,
-                        stop=True,
-                    )
-                y_turned[unit, o] = yt_pool.tile([P, ROWS, P], F32, name="y_turned")
+                nc.tensor.matmul_mx(
+                    out=acc[:],
+                    lhsT=w_codes[:, m, chans].bitcast(FP8X4),
+                    lhsT_scale=w_scales[:, m, chans],
+                    rhs=x_codes[b][:].bitcast(FP8X4),
+                    rhs_scale=x_scales[b][:],
+                    start=True,
+                    stop=True,
+                )
+                y_turned[b, m, o] = yt_pool.tile([P, NB], F32, name="y_turned")
                 nc.scalar.activation(
-                    out=y_turned[unit, o][:],
-                    in_=acc[:, 0:DIRECT_FROM].rearrange("r (q t) -> r t q", t=ROWS),
+                    out=y_turned[b, m, o][:],
+                    in_=acc[:],
                     func=IDENTITY,
                     bias=bias_cols[:, m * O_TILES + o : m * O_TILES + o + 1],
                     scale=1.0 / PIXELS,
                 )
 
         def turn_back(unit):
-            b, m, first = parts_of(unit)
-            if first == 0:
-                y[b, m] = y_pool.tile([P, ROWS, C], F32, name="y")
-            for o in range(first, first + UNIT):
-                back = psum_turn.tile([P, ROWS, P], F32, tag="turned")
-                for t in range(ROWS):
-                    nc.tensor.transpose(back[:, t, :], y_turned[unit, o][:, t, :], identity[:])
+            b, tiles = tiles_of(unit)
+            for m, o in tiles:
+                back = psum_turn.tile([P, N_TILES, P], F32, tag="turned")
+                for t in range(N_TILES):
+                    nc.tensor.transpose(back[:, t, :], y_turned[b, m, o][:, t * P : (t + 1) * P], identity[:])
                 if b == B - 1:
-                    nc.vector.tensor_copy(out=y[b, m][:, :, o * P : (o + 1) * P], in_=back[:])
+                    nc.vector.tensor_copy(out=result(b, m)[:, :, o * P : (o + 1) * P], in_=back[:])
                 else:
-                    nc.scalar.copy(out=y[b, m][:, :, o * P : (o + 1) * P], in_=back[:])
-            out_rows = outs[m][b][0:DIRECT_FROM].rearrange("(q t) c -> q t c", t=ROWS)
+                    nc.scalar.copy(out=result(b, m)[:, :, o * P : (o + 1) * P], in_=back[:])
+            m, o = tiles[UNIT - 1]
             if b == B - 1:
-                chans = slice(first * P, (first + UNIT) * P)
-                nc.sync.dma_start(out=out_rows[:, :, chans], in_=y[b, m][:, :, chans])
-            elif first + UNIT == O_TILES:
-                nc.sync.dma_start(out=out_rows, in_=y[b, m][:])
+                store(b, m, slice((o + 1 - UNIT) * P, (o + 1) * P))
+            elif (m, o) == (0, O_TILES - 1) or (m, o) == TURNED[len(TURNED) - 1]:
+                store(b, m, slice(0, C))
 
-        def project_direct(b, m):
-            acc_direct[b, m] = psum_side.tile([P, C], F32, tag="side", name="acc_direct")
-            nc.tensor.matmul_mx(
-                out=acc_direct[b, m][:],
-                lhsT=x_codes[b][:, DIRECT_FROM:NB].bitcast(FP8X4),
-                lhsT_scale=x_scales[b][:, DIRECT_FROM:NB],
-                rhs=w_codes[:, m, :].bitcast(FP8X4),
-                rhs_scale=w_scales[:, m, :],
-                start=True,
-                stop=True,
-            )
+        def project_direct(b, half):
+            acc_direct[b, half] = psum_direct.tile([P, N_TILES // HALVES, DIRECT_WIDTH], F32, name="acc_direct")
+            for s in range(N_TILES // HALVES):
+                t = half * (N_TILES // HALVES) + s
+                nc.tensor.matmul_mx(
+                    out=acc_direct[b, half][:, s, :],
+                    lhsT=x_codes[b][:, t * P : (t + 1) * P].bitcast(FP8X4),
+                    lhsT_scale=x_scales[b][:, t * P : (t + 1) * P],
+                    rhs=w_codes[:, DIRECT_M, DIRECT_FROM:C].bitcast(FP8X4),
+                    rhs_scale=w_scales[:, DIRECT_M, DIRECT_FROM:C],
+                    start=True,
+                    stop=True,
+                )
 
-        def finish_direct(b, m):
-            y_direct = yd_pool.tile([P, C], F32, name="y_direct")
+        def finish_direct(b, half):
+            ts = slice(half * (N_TILES // HALVES), (half + 1) * (N_TILES // HALVES))
             nc.vector.scalar_tensor_tensor(
-                out=y_direct[:],
-                in0=acc_direct[b, m][:],
+                out=result(b, DIRECT_M)[:, ts, DIRECT_FROM:C],
+                in0=acc_direct[b, half][:],
                 scalar=1.0 / PIXELS,
-                in1=bias_all[:, m, :],
+                in1=bias_direct[:],
                 op0=MULT,
                 op1=ADD,
             )
-            nc.sync.dma_start(out=outs[m][b][DIRECT_FROM:NB, :], in_=y_direct[:])
+            if b == B - 1 and half == HALVES - 1:
+                store(b, DIRECT_M, slice(DIRECT_FROM, C))
 
         load_image(0)
         identity = const.tile([P, P], F32)
@@ -256,13 +266,17 @@ def tile_coarseblockattention_pa_t_kernel(tc, x, Wq, bq, Wk, bk, out_0, out_1):
         nc.tensor.transpose(bias_turned[:], bias_rows_f32[:], identity[:])
         bias_cols = const.tile([P, 2 * O_TILES], F32)
         nc.scalar.copy(out=bias_cols[:], in_=bias_turned[:, 0 : 2 * O_TILES])
-        bias_all = const.tile([P, 2, C], F32)
-        for m in range(2):
-            spread = psum_turn.tile([P, O_TILES, P], F32, tag="turned")
-            for o in range(O_TILES):
-                col = m * O_TILES + o
-                nc.tensor.transpose(spread[:, o, :], bias_cols[:, col : col + 1].to_broadcast([P, P]), identity[:])
-            nc.scalar.copy(out=bias_all[:, m, :], in_=spread[:].rearrange("q o r -> q (o r)"))
+        bias_direct = const.tile([P, N_TILES // HALVES, DIRECT_WIDTH], F32)
+        spread = psum_turn.tile([P, N_TILES // HALVES, DIRECT_WIDTH], F32, tag="turned")
+        for s in range(N_TILES // HALVES):
+            for o in range(DIRECT_FROM // P, O_TILES):
+                col = DIRECT_M * O_TILES + o
+                nc.tensor.transpose(
+                    spread[:, s, o * P - DIRECT_FROM : (o + 1) * P - DIRECT_FROM],
+                    bias_cols[:, col : col + 1].to_broadcast([P, P]),
+                    identity[:],
+                )
+        nc.scalar.copy(out=bias_direct[:], in_=spread[:])
 
         for b in range(B):
             if b + LOADS_AHEAD < B:
@@ -272,19 +286,19 @@ def tile_coarseblockattention_pa_t_kernel(tc, x, Wq, bq, Wk, bk, out_0, out_1):
                     add_rows(b + 1, piece)
             for k in range(UNITS_PER_IMAGE):
                 unit = b * UNITS_PER_IMAGE + k
-                if k == UNITS_PER_IMAGE // 2 and b + 1 < B:
+                if k == UNITS_PER_IMAGE - 1 and b + 1 < B:
                     add_columns(b + 1)
                 project(unit)
                 if k == 0 and b + 1 < B:
                     pool_on_tensor(b + 1)
-                if k % 2 == 0:
-                    project_direct(b, k // 2)
+                if k > 0:
+                    project_direct(b, k - 1)
                 if unit > 0:
                     turn_back(unit - 1)
                 if k == 0 and b + 1 < B:
                     round_pooled(b + 1)
-                if k % 2 == 0:
-                    finish_direct(b, k // 2)
+                if k > 0:
+                    finish_direct(b, k - 1)
             if b + 1 < B:
                 quantise_image(b + 1)
         turn_back(UNITS - 1)

@@ -98,7 +98,10 @@ def tile_coarseblockattention_pa_t_kernel(tc, x, Wq, bq, Wk, bk, out_0, out_1):
                     )
 
         def round_pooled(b):
-            nc.scalar.copy(out=grouped[b][:, TENSOR_POOLS_FROM:NB, :], in_=pooled[b][:].rearrange("p j n -> p n j"))
+            nc.scalar.copy(
+                out=grouped[b][:].rearrange("p (t q) j -> p t q j", t=N_TILES)[:, :, TENSOR_POOLS_FROM // N_TILES : P, :],
+                in_=pooled[b][:].rearrange("p j (q t) -> p t q j", t=N_TILES),
+            )
 
         def add_rows(b, piece):
             if piece == 0:
@@ -115,9 +118,9 @@ def tile_coarseblockattention_pa_t_kernel(tc, x, Wq, bq, Wk, bk, out_0, out_1):
             )
 
         def add_columns(b):
-            halves = row_sums[b][:, :, 0 : 2 * TENSOR_POOLS_FROM].rearrange("p j (g s e) -> p e g j s", s=PACK, e=2)
+            halves = row_sums[b][:, :, 0 : 2 * TENSOR_POOLS_FROM].rearrange("p j (q t e) -> p e q j t", t=N_TILES, e=2)
             nc.vector.tensor_tensor(
-                out=grouped[b][:, 0:TENSOR_POOLS_FROM, :].rearrange("p (g s) j -> p g j s", s=PACK),
+                out=grouped[b][:].rearrange("p (t q) j -> p q j t", t=N_TILES)[:, 0 : TENSOR_POOLS_FROM // N_TILES],
                 in0=halves[:, 0],
                 in1=halves[:, 1],
                 op=ADD,
@@ -165,7 +168,7 @@ def tile_coarseblockattention_pa_t_kernel(tc, x, Wq, bq, Wk, bk, out_0, out_1):
             return y[b, m]
 
         def store(b, m, chans):
-            out_rows = outs[m][b].rearrange("(t q) c -> q t c", q=P)
+            out_rows = outs[m][b].rearrange("(q t) c -> q t c", q=P)
             nc.sync.dma_start(out=out_rows[:, :, chans], in_=result(b, m)[:, :, chans])
 
         def tiles_of(unit):

@@ -29,12 +29,14 @@ DIRECT_WIDTH = C - DIRECT_FROM
 HALVES = 2
 LOADS_AHEAD = 4
 FIRST_PIECES = 4
-PIECES = 2
+SECOND_PIECES = 2
+PIECES = 1
 UNIT = 2
 UNITS_PER_IMAGE = len(TURNED) // UNIT
 UNITS = B * UNITS_PER_IMAGE
 ACC_BANKS = 3
-TURN_BANKS = 2
+TURN_BANKS = 3
+SIDE_BANKS = 2
 
 FLOPS = 2 * 2 * B * NB * C * C
 
@@ -53,8 +55,7 @@ def tile_coarseblockattention_pa_t_kernel(tc, x, Wq, bq, Wk, bk, out_0, out_1):
         y_pool = ctx.enter_context(tc.tile_pool(name="y_pool", bufs=6))
         psum_acc = ctx.enter_context(tc.psum_pool(name="psum_acc", bufs=ACC_BANKS))
         psum_turn = ctx.enter_context(tc.psum_pool(name="psum_turn", bufs=TURN_BANKS))
-        psum_direct = ctx.enter_context(tc.psum_pool(name="psum_direct", bufs=HALVES))
-        psum_pooled = ctx.enter_context(tc.psum_pool(name="psum_pooled", bufs=1))
+        psum_side = ctx.enter_context(tc.psum_pool(name="psum_side", bufs=SIDE_BANKS))
         ctx.enter_context(tc.manual_schedule())
 
         x_sb = {}
@@ -63,13 +64,14 @@ def tile_coarseblockattention_pa_t_kernel(tc, x, Wq, bq, Wk, bk, out_0, out_1):
         x_codes = {}
         x_scales = {}
         w_rows = {}
+        w_grouped = {}
         y_turned = {}
         y = {}
         acc_direct = {}
         pooled = {}
 
         def pieces_of(b):
-            return FIRST_PIECES if b == 0 else PIECES
+            return (FIRST_PIECES, SECOND_PIECES)[b] if b < 2 else PIECES
 
         def channels_of(b, piece):
             width = PACK // pieces_of(b)
@@ -83,7 +85,7 @@ def tile_coarseblockattention_pa_t_kernel(tc, x, Wq, bq, Wk, bk, out_0, out_1):
                 nc.sync.dma_start(out=x_sb[b][:, js, :], in_=x_b[:, js, :])
 
         def pool_on_tensor(b):
-            pooled[b] = psum_pooled.tile([P, PACK, NB - TENSOR_POOLS_FROM], F32, name="pooled")
+            pooled[b] = psum_side.tile([P, PACK, NB - TENSOR_POOLS_FROM], F32, tag="side", name="pooled")
             pixels = x_sb[b][:, :, PIXELS * TENSOR_POOLS_FROM : PIXELS * NB].rearrange(
                 "p j (v i w e) -> p i e j v w", i=2, w=W // 2, e=2
             )
@@ -98,6 +100,7 @@ def tile_coarseblockattention_pa_t_kernel(tc, x, Wq, bq, Wk, bk, out_0, out_1):
                     )
 
         def round_pooled(b):
+            grouped[b] = work.tile([P, NB, PACK], BF16, align_bytes=64, name="grouped")
             nc.scalar.copy(
                 out=grouped[b][:].rearrange("p (t q) j -> p t q j", t=N_TILES)[:, :, TENSOR_POOLS_FROM // N_TILES : P, :],
                 in_=pooled[b][:].rearrange("p j (q t) -> p t q j", t=N_TILES),
@@ -106,7 +109,6 @@ def tile_coarseblockattention_pa_t_kernel(tc, x, Wq, bq, Wk, bk, out_0, out_1):
         def add_rows(b, piece):
             if piece == 0:
                 row_sums[b] = work.tile([P, PACK, BLOCK_ROWS * W], F32, name="row_sums")
-                grouped[b] = work.tile([P, NB, PACK], BF16, align_bytes=64, name="grouped")
             js = channels_of(b, piece)
             block_rows = TENSOR_POOLS_FROM // (W // 2)
             rows = x_sb[b][:, js, 0 : block_rows * 2 * W].rearrange("p j (v i w) -> p j v i w", i=2, w=W)
@@ -136,30 +138,34 @@ def tile_coarseblockattention_pa_t_kernel(tc, x, Wq, bq, Wk, bk, out_0, out_1):
             )
 
         def load_weight(m):
-            w_rows[m] = w_stage.tile([P, O_TILES, C], BF16, name="w_rows")
-            nc.sync.dma_start(out=w_rows[m][:], in_=weights[m].rearrange("(o r) c -> r o c", r=P))
+            w_rows[m] = w_stage.tile([P, PACK, C], BF16, name="w_rows")
+            nc.sync.dma_start(out=w_rows[m][:], in_=weights[m].rearrange("(r s) c -> r s c", s=PACK))
+
+        def load_bias(m):
             nc.sync.dma_start(
                 out=bias_rows[m * O_TILES : (m + 1) * O_TILES, :],
                 in_=biases[m].rearrange("(o r) -> o r", r=P),
             )
 
-        def quantise_weight(m):
-            w_words = w_rows[m][:].bitcast(F32).rearrange("r o (p u) -> r o u p", u=WORDS)
-            w_grouped = w_stage.tile([P, C, PACK], BF16, align_bytes=64)
-            grouped_words = w_grouped[:].bitcast(F32).rearrange("p (o r) u -> p o r u", r=P)
-            for pair in range(O_TILES // 2):
+        def turn_weight(m):
+            w_words = w_rows[m][:].bitcast(F32).rearrange("r s (p u) -> r s u p", u=WORDS)
+            w_grouped[m] = w_stage.tile([P, C, PACK], BF16, align_bytes=64, name="w_grouped")
+            grouped_words = w_grouped[m][:].bitcast(F32).rearrange("p (r s) u -> p r s u", s=PACK)
+            for pair in range(PACK // 2):
                 turned = psum_turn.tile([P, 2, WORDS, P], F32, tag="turned")
-                for o in range(2):
+                for s in range(2):
                     for u in range(WORDS):
-                        nc.tensor.transpose(turned[:, o, u, :], w_words[:, 2 * pair + o, u, :], identity[:])
+                        nc.tensor.transpose(turned[:, s, u, :], w_words[:, 2 * pair + s, u, :], identity[:])
                 nc.scalar.copy(
-                    out=grouped_words[:, 2 * pair : 2 * pair + 2],
-                    in_=turned[:].rearrange("p o u r -> p o r u"),
+                    out=grouped_words[:, :, 2 * pair : 2 * pair + 2, :],
+                    in_=turned[:].rearrange("p s u r -> p r s u"),
                 )
+
+        def quantise_weight(m):
             nc.vector.quantize_mx(
                 out=w_codes[:, m, :].bitcast(FP8X4),
                 scales=w_scales[:, m, :],
-                in_=w_grouped[:].rearrange("p c j -> p (c j)"),
+                in_=w_grouped[m][:].rearrange("p c j -> p (c j)"),
             )
 
         def result(b, m):
@@ -167,9 +173,11 @@ def tile_coarseblockattention_pa_t_kernel(tc, x, Wq, bq, Wk, bk, out_0, out_1):
                 y[b, m] = y_pool.tile([P, N_TILES, C], F32, name="y")
             return y[b, m]
 
-        def store(b, m, chans):
-            out_rows = outs[m][b].rearrange("(q t) c -> q t c", q=P)
-            nc.sync.dma_start(out=out_rows[:, :, chans], in_=result(b, m)[:, :, chans])
+        def store(b, m):
+            nc.sync.dma_start(out=outs[m][b].rearrange("(q t) c -> q t c", q=P), in_=result(b, m)[:])
+
+        def on_vector(b, o):
+            return b == B - 1 and o % 2 == 1
 
         def tiles_of(unit):
             first = unit % UNITS_PER_IMAGE * UNIT
@@ -190,13 +198,23 @@ def tile_coarseblockattention_pa_t_kernel(tc, x, Wq, bq, Wk, bk, out_0, out_1):
                     stop=True,
                 )
                 y_turned[b, m, o] = yt_pool.tile([P, NB], F32, name="y_turned")
-                nc.scalar.activation(
-                    out=y_turned[b, m, o][:],
-                    in_=acc[:],
-                    func=IDENTITY,
-                    bias=bias_cols[:, m * O_TILES + o : m * O_TILES + o + 1],
-                    scale=1.0 / PIXELS,
-                )
+                if on_vector(b, o):
+                    nc.vector.tensor_scalar(
+                        out=y_turned[b, m, o][:],
+                        in0=acc[:],
+                        scalar1=1.0 / PIXELS,
+                        scalar2=bias_cols[:, m * O_TILES + o : m * O_TILES + o + 1],
+                        op0=MULT,
+                        op1=ADD,
+                    )
+                else:
+                    nc.scalar.activation(
+                        out=y_turned[b, m, o][:],
+                        in_=acc[:],
+                        func=IDENTITY,
+                        bias=bias_cols[:, m * O_TILES + o : m * O_TILES + o + 1],
+                        scale=1.0 / PIXELS,
+                    )
 
         def turn_back(unit):
             b, tiles = tiles_of(unit)
@@ -204,18 +222,16 @@ def tile_coarseblockattention_pa_t_kernel(tc, x, Wq, bq, Wk, bk, out_0, out_1):
                 back = psum_turn.tile([P, N_TILES, P], F32, tag="turned")
                 for t in range(N_TILES):
                     nc.tensor.transpose(back[:, t, :], y_turned[b, m, o][:, t * P : (t + 1) * P], identity[:])
-                if b == B - 1:
+                if on_vector(b, o):
                     nc.vector.tensor_copy(out=result(b, m)[:, :, o * P : (o + 1) * P], in_=back[:])
                 else:
                     nc.scalar.copy(out=result(b, m)[:, :, o * P : (o + 1) * P], in_=back[:])
             m, o = tiles[UNIT - 1]
-            if b == B - 1:
-                store(b, m, slice((o + 1 - UNIT) * P, (o + 1) * P))
-            elif (m, o) == (0, O_TILES - 1) or (m, o) == TURNED[len(TURNED) - 1]:
-                store(b, m, slice(0, C))
+            if (m, o) == (0, O_TILES - 1) or (m, o) == TURNED[len(TURNED) - 1]:
+                store(b, m)
 
         def project_direct(b, half):
-            acc_direct[b, half] = psum_direct.tile([P, N_TILES // HALVES, DIRECT_WIDTH], F32, name="acc_direct")
+            acc_direct[b, half] = psum_side.tile([P, N_TILES // HALVES, DIRECT_WIDTH], F32, tag="side", name="acc_direct")
             for s in range(N_TILES // HALVES):
                 t = half * (N_TILES // HALVES) + s
                 nc.tensor.matmul_mx(
@@ -238,10 +254,7 @@ def tile_coarseblockattention_pa_t_kernel(tc, x, Wq, bq, Wk, bk, out_0, out_1):
                 op0=MULT,
                 op1=ADD,
             )
-            if b == B - 1 and half == HALVES - 1:
-                store(b, DIRECT_M, slice(DIRECT_FROM, C))
 
-        load_image(0)
         identity = const.tile([P, P], F32)
         masks.make_identity(nc, identity[:])
         identity_bf16 = const.tile([P, P], BF16)
@@ -251,18 +264,14 @@ def tile_coarseblockattention_pa_t_kernel(tc, x, Wq, bq, Wk, bk, out_0, out_1):
         bias_rows = const.tile([P, P], BF16)
         nc.vector.memset(bias_rows[:], 0.0)
         load_weight(0)
+        load_bias(0)
+        load_bias(1)
+        load_image(0)
         load_weight(1)
         for b in range(1, LOADS_AHEAD):
             load_image(b)
 
-        for piece in range(pieces_of(0)):
-            add_rows(0, piece)
-        pool_on_tensor(0)
-        round_pooled(0)
-        add_columns(0)
-        quantise_weight(0)
-        quantise_image(0)
-        quantise_weight(1)
+        turn_weight(0)
         bias_rows_f32 = const.tile([P, P], F32)
         nc.scalar.copy(out=bias_rows_f32[:], in_=bias_rows[:])
         bias_turned = psum_turn.tile([P, P], F32, tag="turned")
@@ -280,28 +289,47 @@ def tile_coarseblockattention_pa_t_kernel(tc, x, Wq, bq, Wk, bk, out_0, out_1):
                     identity[:],
                 )
         nc.scalar.copy(out=bias_direct[:], in_=spread[:])
+        add_rows(0, 0)
+        add_rows(0, 1)
+        quantise_weight(0)
+        add_rows(0, 2)
+        add_rows(0, 3)
+        pool_on_tensor(0)
+        round_pooled(0)
+        add_columns(0)
+        turn_weight(1)
+        quantise_image(0)
+        quantise_weight(1)
 
         for b in range(B):
             if b + LOADS_AHEAD < B:
                 load_image(b + LOADS_AHEAD)
+            first = b * UNITS_PER_IMAGE
             if b + 1 < B:
-                for piece in range(pieces_of(b + 1)):
+                add_rows(b + 1, 0)
+            project(first)
+            project_direct(b, 0)
+            if b > 0 and b + 1 < B:
+                for piece in range(1, pieces_of(b + 1)):
                     add_rows(b + 1, piece)
-            for k in range(UNITS_PER_IMAGE):
-                unit = b * UNITS_PER_IMAGE + k
-                if k == UNITS_PER_IMAGE - 1 and b + 1 < B:
-                    add_columns(b + 1)
-                project(unit)
-                if k == 0 and b + 1 < B:
-                    pool_on_tensor(b + 1)
-                if k > 0:
-                    project_direct(b, k - 1)
-                if unit > 0:
-                    turn_back(unit - 1)
-                if k == 0 and b + 1 < B:
-                    round_pooled(b + 1)
-                if k > 0:
-                    finish_direct(b, k - 1)
+            finish_direct(b, 0)
+            if b == 0:
+                for piece in range(1, pieces_of(1)):
+                    add_rows(1, piece)
+            project(first + 1)
+            project_direct(b, 1)
+            turn_back(first)
+            if b == 0:
+                pool_on_tensor(1)
+                round_pooled(1)
+            if b + 1 < B:
+                add_columns(b + 1)
+            project(first + 2)
+            turn_back(first + 1)
+            finish_direct(b, 1)
+            if b + 2 < B:
+                pool_on_tensor(b + 2)
+                round_pooled(b + 2)
+            turn_back(first + 2)
             if b + 1 < B:
                 quantise_image(b + 1)
-        turn_back(UNITS - 1)

@@ -28,6 +28,7 @@ DIRECT_FROM = 2 * P
 DIRECT_WIDTH = C - DIRECT_FROM
 HALVES = 2
 LOADS_AHEAD = 4
+PAIRED_STORES = 4
 FIRST_PIECES = 4
 SECOND_PIECES = 2
 PIECES = 1
@@ -52,7 +53,7 @@ def tile_coarseblockattention_pa_t_kernel(tc, x, Wq, bq, Wk, bk, out_0, out_1):
         x_pool = ctx.enter_context(tc.tile_pool(name="x_pool", bufs=LOADS_AHEAD + 1))
         work = ctx.enter_context(tc.tile_pool(name="work", bufs=2))
         yt_pool = ctx.enter_context(tc.tile_pool(name="yt_pool", bufs=3 * UNIT))
-        y_pool = ctx.enter_context(tc.tile_pool(name="y_pool", bufs=6))
+        y_pool = ctx.enter_context(tc.tile_pool(name="y_pool", bufs=5))
         psum_acc = ctx.enter_context(tc.psum_pool(name="psum_acc", bufs=ACC_BANKS))
         psum_turn = ctx.enter_context(tc.psum_pool(name="psum_turn", bufs=TURN_BANKS))
         psum_side = ctx.enter_context(tc.psum_pool(name="psum_side", bufs=SIDE_BANKS))
@@ -108,7 +109,7 @@ def tile_coarseblockattention_pa_t_kernel(tc, x, Wq, bq, Wk, bk, out_0, out_1):
 
         def add_rows(b, piece):
             if piece == 0:
-                row_sums[b] = work.tile([P, PACK, BLOCK_ROWS * W], F32, name="row_sums")
+                row_sums[b] = work.tile([P, PACK, 2 * TENSOR_POOLS_FROM], F32, name="row_sums")
             js = channels_of(b, piece)
             block_rows = TENSOR_POOLS_FROM // (W // 2)
             rows = x_sb[b][:, js, 0 : block_rows * 2 * W].rearrange("p j (v i w) -> p j v i w", i=2, w=W)
@@ -169,12 +170,25 @@ def tile_coarseblockattention_pa_t_kernel(tc, x, Wq, bq, Wk, bk, out_0, out_1):
             )
 
         def result(b, m):
-            if (b, m) not in y:
-                y[b, m] = y_pool.tile([P, N_TILES, C], F32, name="y")
-            return y[b, m]
+            k = b // 2
+            if (k, m) not in y:
+                for each_m in range(2):
+                    y[k, each_m] = y_pool.tile([P, 2, N_TILES, C], F32, name="y")
+            return y[k, m][:, b % 2]
 
         def store(b, m):
-            nc.sync.dma_start(out=outs[m][b].rearrange("(q t) c -> q t c", q=P), in_=result(b, m)[:])
+            if b >= PAIRED_STORES:
+                images = slice(b, b + 1)
+            elif b % 2 == 1:
+                images = slice(b - 1, b + 1)
+            else:
+                return
+            nc.sync.dma_start(
+                out=outs[m][images].rearrange("i (q t) c -> q i (t c)", q=P),
+                in_=y[b // 2, m][:, images.start % 2 : images.start % 2 + images.stop - images.start].rearrange(
+                    "q i t c -> q i (t c)"
+                ),
+            )
 
         def on_vector(b, o):
             return b == B - 1 and o % 2 == 1

from contextlib import ExitStack

import concourse.masks as masks
import concourse.mybir as mybir

BF16 = mybir.dt.bfloat16
F32 = mybir.dt.float32
U32 = mybir.dt.uint32
U8 = mybir.dt.uint8
FP8X4 = mybir.dt.float8_e4m3fn_x4
ADD = mybir.AluOpType.add
MULT = mybir.AluOpType.mult
IDENTITY = mybir.ActivationFunctionType.Identity

P = 128
PACK = 4
WORDS = 2
B, C, H, W = 8, 512, 64, 32
PIXELS = 4
BLOCK_ROWS = H // 2
NB = BLOCK_ROWS * (W // 2)
N_TILES = NB // P
O_TILES = C // P
TENSOR_POOLS_FROM = NB - 96
TURNED = ((0, 0), (0, 1), (0, 2), (0, 3), (1, 0), (1, 1))
DIRECT_M = 1
DIRECT_FROM = 2 * P
DIRECT_WIDTH = C - DIRECT_FROM
HALVES = 2
LOADS_AHEAD = 4
PAIRED_STORES = 4
FIRST_PIECES = 4
SECOND_PIECES = 2
PIECES = 1
UNIT = 2
UNITS_PER_IMAGE = len(TURNED) // UNIT
UNITS = B * UNITS_PER_IMAGE
ACC_BANKS = 3
TURN_BANKS = 3
SIDE_BANKS = 2

FLOPS = 2 * 2 * B * NB * C * C


def tile_coarseblockattention_pa_t_kernel(tc, x, Wq, bq, Wk, bk, out_0, out_1):
    nc = tc.nc
    weights = (Wq, Wk)
    biases = (bq, bk)
    outs = (out_0, out_1)
    with ExitStack() as ctx:
        const = ctx.enter_context(tc.tile_pool(name="const", bufs=1))
        w_stage = ctx.enter_context(tc.tile_pool(name="w_stage", bufs=2))
        x_pool = ctx.enter_context(tc.tile_pool(name="x_pool", bufs=LOADS_AHEAD + 1))
        work = ctx.enter_context(tc.tile_pool(name="work", bufs=2))
        yt_pool = ctx.enter_context(tc.tile_pool(name="yt_pool", bufs=3 * UNIT))
        y_pool = ctx.enter_context(tc.tile_pool(name="y_pool", bufs=5))
        psum_acc = ctx.enter_context(tc.psum_pool(name="psum_acc", bufs=ACC_BANKS))
        psum_turn = ctx.enter_context(tc.psum_pool(name="psum_turn", bufs=TURN_BANKS))
        psum_side = ctx.enter_context(tc.psum_pool(name="psum_side", bufs=SIDE_BANKS))
        ctx.enter_context(tc.manual_schedule())

        x_sb = {}
        row_sums = {}
        grouped = {}
        x_codes = {}
        x_scales = {}
        w_rows = {}
        w_grouped = {}
        y_turned = {}
        y = {}
        acc_direct = {}
        pooled = {}

        def pieces_of(b):
            return (FIRST_PIECES, SECOND_PIECES)[b] if b < 2 else PIECES

        def channels_of(b, piece):
            width = PACK // pieces_of(b)
            return slice(piece * width, (piece + 1) * width)

        def load_image(b):
            x_sb[b] = x_pool.tile([P, PACK, H * W], BF16, name="x_sb")
            x_b = x[b].rearrange("(p j) h w -> p j (h w)", j=PACK)
            for piece in range(pieces_of(b)):
                js = channels_of(b, piece)
                nc.sync.dma_start(out=x_sb[b][:, js, :], in_=x_b[:, js, :])

        def pool_on_tensor(b):
            pooled[b] = psum_side.tile([P, PACK, NB - TENSOR_POOLS_FROM], F32, tag="side", name="pooled")
            pixels = x_sb[b][:, :, PIXELS * TENSOR_POOLS_FROM : PIXELS * NB].rearrange(
                "p j (v i w e) -> p i e j v w", i=2, w=W // 2, e=2
            )
            for i in range(2):
                for e in range(2):
                    nc.tensor.matmul(
                        out=pooled[b][:].rearrange("p j n -> p (j n)"),
                        lhsT=identity_bf16[:],
                        rhs=pixels[:, i, e],
                        start=(i == 0 and e == 0),
                        stop=(i == 1 and e == 1),
                    )

        def round_pooled(b):
            grouped[b] = work.tile([P, NB, PACK], BF16, align_bytes=64, name="grouped")
            nc.scalar.copy(
                out=grouped[b][:].rearrange("p (t q) j -> p t q j", t=N_TILES)[:, :, TENSOR_POOLS_FROM // N_TILES : P, :],
                in_=pooled[b][:].rearrange("p j (q t) -> p t q j", t=N_TILES),
            )

        def add_rows(b, piece):
            if piece == 0:
                row_sums[b] = work.tile([P, PACK, 2 * TENSOR_POOLS_FROM], F32, name="row_sums")
            js = channels_of(b, piece)
            block_rows = TENSOR_POOLS_FROM // (W // 2)
            rows = x_sb[b][:, js, 0 : block_rows * 2 * W].rearrange("p j (v i w) -> p j v i w", i=2, w=W)
            nc.vector.tensor_tensor(
                out=row_sums[b][:, js, 0 : block_rows * W].rearrange("p j (v w) -> p j v w", w=W),
                in0=rows[:, :, :, 0, :],
                in1=rows[:, :, :, 1, :],
                op=ADD,
            )

        def add_columns(b):
            halves = row_sums[b][:, :, 0 : 2 * TENSOR_POOLS_FROM].rearrange("p j (q t e) -> p e q j t", t=N_TILES, e=2)
            nc.vector.tensor_tensor(
                out=grouped[b][:].rearrange("p (t q) j -> p q j t", t=N_TILES)[:, 0 : TENSOR_POOLS_FROM // N_TILES],
                in0=halves[:, 0],
                in1=halves[:, 1],
                op=ADD,
            )

        def quantise_image(b):
            x_codes[b] = work.tile([P, NB], U32, align_bytes=64, name="x_codes")
            x_scales[b] = work.tile([P, NB], U8, align_bytes=64, name="x_scales")
            nc.vector.quantize_mx(
                out=x_codes[b][:].bitcast(FP8X4),
                scales=x_scales[b][:],
                in_=grouped[b][:].rearrange("p n j -> p (n j)"),
            )

        def load_weight(m):
            w_rows[m] = w_stage.tile([P, PACK, C], BF16, name="w_rows")
            nc.sync.dma_start(out=w_rows[m][:], in_=weights[m].rearrange("(r s) c -> r s c", s=PACK))

        def load_bias(m):
            nc.sync.dma_start(
                out=bias_rows[m * O_TILES : (m + 1) * O_TILES, :],
                in_=biases[m].rearrange("(o r) -> o r", r=P),
            )

        def turn_weight(m):
            w_words = w_rows[m][:].bitcast(F32).rearrange("r s (p u) -> r s u p", u=WORDS)
            w_grouped[m] = w_stage.tile([P, C, PACK], BF16, align_bytes=64, name="w_grouped")
            grouped_words = w_grouped[m][:].bitcast(F32).rearrange("p (r s) u -> p r s u", s=PACK)
            for pair in range(PACK // 2):
                turned = psum_turn.tile([P, 2, WORDS, P], F32, tag="turned")
                for s in range(2):
                    for u in range(WORDS):
                        nc.tensor.transpose(turned[:, s, u, :], w_words[:, 2 * pair + s, u, :], identity[:])
                nc.scalar.copy(
                    out=grouped_words[:, :, 2 * pair : 2 * pair + 2, :],
                    in_=turned[:].rearrange("p s u r -> p r s u"),
                )

        def quantise_weight(m):
            nc.vector.quantize_mx(
                out=w_codes[:, m, :].bitcast(FP8X4),
                scales=w_scales[:, m, :],
                in_=w_grouped[m][:].rearrange("p c j -> p (c j)"),
            )

        def result(b, m):
            k = b // 2
            if (k, m) not in y:
                for each_m in range(2):
                    y[k, each_m] = y_pool.tile([P, 2, N_TILES, C], F32, name="y")
            return y[k, m][:, b % 2]

        def store(b, m):
            if b >= PAIRED_STORES:
                images = slice(b, b + 1)
            elif b % 2 == 1:
                images = slice(b - 1, b + 1)
            else:
                return
            nc.sync.dma_start(
                out=outs[m][images].rearrange("i (q t) c -> q i (t c)", q=P),
                in_=y[b // 2, m][:, images.start % 2 : images.start % 2 + images.stop - images.start].rearrange(
                    "q i t c -> q i (t c)"
                ),
            )

        def on_vector(b, o):
            return b == B - 1 and o % 2 == 1

        def tiles_of(unit):
            first = unit % UNITS_PER_IMAGE * UNIT
            return unit // UNITS_PER_IMAGE, TURNED[first : first + UNIT]

        def project(unit):
            b, tiles = tiles_of(unit)
            for m, o in tiles:
                chans = slice(o * P, (o + 1) * P)
                acc = psum_acc.tile([P, NB], F32)
                nc.tensor.matmul_mx(
                    out=acc[:],
                    lhsT=w_codes[:, m, chans].bitcast(FP8X4),
                    lhsT_scale=w_scales[:, m, chans],
                    rhs=x_codes[b][:].bitcast(FP8X4),
                    rhs_scale=x_scales[b][:],
                    start=True,
                    stop=True,
                )
                y_turned[b, m, o] = yt_pool.tile([P, NB], F32, name="y_turned")
                if on_vector(b, o):
                    nc.vector.tensor_scalar(
                        out=y_turned[b, m, o][:],
                        in0=acc[:],
                        scalar1=1.0 / PIXELS,
                        scalar2=bias_cols[:, m * O_TILES + o : m * O_TILES + o + 1],
                        op0=MULT,
                        op1=ADD,
                    )
                else:
                    nc.scalar.activation(
                        out=y_turned[b, m, o][:],
                        in_=acc[:],
                        func=IDENTITY,
                        bias=bias_cols[:, m * O_TILES + o : m * O_TILES + o + 1],
                        scale=1.0 / PIXELS,
                    )

        def turn_back(unit):
            b, tiles = tiles_of(unit)
            for m, o in tiles:
                back = psum_turn.tile([P, N_TILES, P], F32, tag="turned")
                for t in range(N_TILES):
                    nc.tensor.transpose(back[:, t, :], y_turned[b, m, o][:, t * P : (t + 1) * P], identity[:])
                if on_vector(b, o):
                    nc.vector.tensor_copy(out=result(b, m)[:, :, o * P : (o + 1) * P], in_=back[:])
                else:
                    nc.scalar.copy(out=result(b, m)[:, :, o * P : (o + 1) * P], in_=back[:])
            m, o = tiles[UNIT - 1]
            if (m, o) == (0, O_TILES - 1) or (m, o) == TURNED[len(TURNED) - 1]:
                store(b, m)

        def project_direct(b, half):
            acc_direct[b, half] = psum_side.tile([P, N_TILES // HALVES, DIRECT_WIDTH], F32, tag="side", name="acc_direct")
            for s in range(N_TILES // HALVES):
                t = half * (N_TILES // HALVES) + s
                nc.tensor.matmul_mx(
                    out=acc_direct[b, half][:, s, :],
                    lhsT=x_codes[b][:, t * P : (t + 1) * P].bitcast(FP8X4),
                    lhsT_scale=x_scales[b][:, t * P : (t + 1) * P],
                    rhs=w_codes[:, DIRECT_M, DIRECT_FROM:C].bitcast(FP8X4),
                    rhs_scale=w_scales[:, DIRECT_M, DIRECT_FROM:C],
                    start=True,
                    stop=True,
                )

        def finish_direct(b, half):
            ts = slice(half * (N_TILES // HALVES), (half + 1) * (N_TILES // HALVES))
            nc.vector.scalar_tensor_tensor(
                out=result(b, DIRECT_M)[:, ts, DIRECT_FROM:C],
                in0=acc_direct[b, half][:],
                scalar=1.0 / PIXELS,
                in1=bias_direct[:],
                op0=MULT,
                op1=ADD,
            )

        identity = const.tile([P, P], F32)
        masks.make_identity(nc, identity[:])
        identity_bf16 = const.tile([P, P], BF16)
        masks.make_identity(nc, identity_bf16[:])
        w_codes = const.tile([P, 2, C], U32, align_bytes=64)
        w_scales = const.tile([P, 2, C], U8, align_bytes=64)
        bias_rows = const.tile([P, P], BF16)
        nc.vector.memset(bias_rows[:], 0.0)
        load_weight(0)
        load_bias(0)
        load_bias(1)
        load_image(0)
        load_weight(1)
        for b in range(1, LOADS_AHEAD):
            load_image(b)

        turn_weight(0)
        bias_rows_f32 = const.tile([P, P], F32)
        nc.scalar.copy(out=bias_rows_f32[:], in_=bias_rows[:])
        bias_turned = psum_turn.tile([P, P], F32, tag="turned")
        nc.tensor.transpose(bias_turned[:], bias_rows_f32[:], identity[:])
        bias_cols = const.tile([P, 2 * O_TILES], F32)
        nc.scalar.copy(out=bias_cols[:], in_=bias_turned[:, 0 : 2 * O_TILES])
        bias_direct = const.tile([P, N_TILES // HALVES, DIRECT_WIDTH], F32)
        spread = psum_turn.tile([P, N_TILES // HALVES, DIRECT_WIDTH], F32, tag="turned")
        for s in range(N_TILES // HALVES):
            for o in range(DIRECT_FROM // P, O_TILES):
                col = DIRECT_M * O_TILES + o
                nc.tensor.transpose(
                    spread[:, s, o * P - DIRECT_FROM : (o + 1) * P - DIRECT_FROM],
                    bias_cols[:, col : col + 1].to_broadcast([P, P]),
                    identity[:],
                )
        nc.scalar.copy(out=bias_direct[:], in_=spread[:])
        add_rows(0, 0)
        add_rows(0, 1)
        quantise_weight(0)
        add_rows(0, 2)
        add_rows(0, 3)
        pool_on_tensor(0)
        round_pooled(0)
        add_columns(0)
        turn_weight(1)
        quantise_image(0)
        quantise_weight(1)

        for b in range(B):
            if b + LOADS_AHEAD < B:
                load_image(b + LOADS_AHEAD)
            first = b * UNITS_PER_IMAGE
            if b + 1 < B:
                add_rows(b + 1, 0)
            project(first)
            project_direct(b, 0)
            if b > 0 and b + 1 < B:
                for piece in range(1, pieces_of(b + 1)):
                    add_rows(b + 1, piece)
            finish_direct(b, 0)
            if b == 0:
                for piece in range(1, pieces_of(1)):
                    add_rows(1, piece)
            project(first + 1)
            project_direct(b, 1)
            turn_back(first)
            if b == 0:
                pool_on_tensor(1)
                round_pooled(1)
            if b + 1 < B:
                add_columns(b + 1)
            project(first + 2)
            turn_back(first + 1)
            finish_direct(b, 1)
            if b + 2 < B:
                pool_on_tensor(b + 2)
                round_pooled(b + 2)
            turn_back(first + 2)
            if b + 1 < B:
                quantise_image(b + 1)
